import numpy as np
import ml_dtypes


def mxq(x, axis, fmt="e4m3"):
    dtype, down = {"e4m3": (ml_dtypes.float8_e4m3fn, 7), "e5m2": (ml_dtypes.float8_e5m2, 14)}[fmt]
    v = np.moveaxis(np.asarray(x, np.float32).astype(ml_dtypes.bfloat16).astype(np.float64), axis, -1)
    blocks = v.reshape(v.shape[:-1] + (-1, 32))
    amax = np.abs(blocks).max(-1, keepdims=True)
    byte = np.maximum(np.where(amax > 0, np.frexp(amax)[1] - 1 + 127, 0) - down, 1)
    scale = np.exp2(byte - 127.0)
    codes = (blocks / scale).astype(np.float32).astype(dtype).astype(np.float64)
    return np.moveaxis((codes * scale).reshape(v.shape), -1, axis)


WIDE = False


def mx_kscale(k):
    if not WIDE:
        return np.ones(k)
    levels = np.array([10, -10, 5, -5, 0])
    a = np.random.permutation(np.resize(levels, k // 512 * 4)).reshape(k // 512, 4)
    idx = np.arange(k)
    return np.exp2(a[idx // 512, idx % 128 // 32])


BF16 = ml_dtypes.bfloat16


def bf(x):
    return np.asarray(x, np.float32).astype(BF16)


def f64(x):
    return np.asarray(x).astype(np.float64)


B, H, S, D = 2, 4, 512, 256
NEG_MIN = -3.4028234663852886e38


def setup_inputs():
    s = mx_kscale(S)
    q = np.random.standard_normal((B, H, S, D)) * 1.4
    k = np.random.standard_normal((B, H, S, D)) * 1.4
    v = np.random.standard_normal((B, H, S, D))
    q[..., 0] = np.log(2.0) * np.sqrt(D)
    k[..., 0] = k[..., 0] + np.log2(s)
    v = v / s[:, None] * s.mean()
    return {"query": bf(q), "key": bf(k), "value": bf(v),
            "attention_mask": bf(np.random.random((B, 1, 1, S)) < 0.75)}


def reference(query, key, value, attention_mask):
    scale = 1.0 / np.sqrt(D)
    scores = (f64(query) @ f64(key).transpose(0, 1, 3, 2)) * scale
    mask_bias = (1.0 - f64(attention_mask)) * NEG_MIN
    z = scores + mask_bias
    e = np.exp(z - z.max(-1, keepdims=True))
    probs = e / e.sum(-1, keepdims=True)
    return mxq(probs, 3, "e4m3") @ mxq(f64(value), 2, "e4m3")

@@ -1,0 +1,264 @@
+from contextlib import ExitStack
+
+import concourse.mybir as mybir
+from concourse.masks import make_identity
+
+F32 = mybir.dt.float32
+BF16 = mybir.dt.bfloat16
+U32 = mybir.dt.uint32
+U8 = mybir.dt.uint8
+FP8X4 = mybir.dt.float8_e4m3fn_x4
+ALU = mybir.AluOpType
+ACT = mybir.ActivationFunctionType
+AXIS = mybir.AxisListType
+
+P = 128
+PACK = 4
+BATCH, HEADS, SEQ, DIM = 2, 4, 512, 256
+N_HEADS = BATCH * HEADS
+Q_TILES = SEQ // P
+N_TILES = N_HEADS * Q_TILES
+N_PAIRS = N_TILES // 2
+SCALE = 1.0 / 16.0
+NEG_MIN = -3.4028234663852886e38
+
+FLOPS = 2 * (2 * N_HEADS * SEQ * SEQ * DIM)
+
+PREP_STEPS = 5
+DRAIN_STEPS = 8
+
+
+def tile_scaleddotproductattention_t_kernel(tc, query, key, value, attention_mask, out):
+    nc = tc.nc
+
+    q_rows = query.rearrange("b h (p t) d -> (b h) p (t d)", t=PACK)
+    k_rows = key.rearrange("b h (p j) d -> (b h) p (j d)", j=PACK)
+    v_rows = value.rearrange("b h (p j) d -> (b h) p (j d)", j=PACK)
+    out_rows = out.rearrange("b h (p t) d -> (b h) p t d", t=PACK)
+
+    with ExitStack() as ctx:
+        ctx.enter_context(tc.manual_schedule())
+        consts = ctx.enter_context(tc.tile_pool(name="consts", bufs=1))
+        inputs = ctx.enter_context(tc.tile_pool(name="inputs", bufs=N_HEADS))
+        transposed = ctx.enter_context(tc.tile_pool(name="transposed", bufs=2))
+        work = ctx.enter_context(tc.tile_pool(name="work", bufs=3))
+        stats = ctx.enter_context(tc.tile_pool(name="stats", bufs=3))
+        packed = ctx.enter_context(tc.tile_pool(name="packed", bufs=2))
+        v_packed = ctx.enter_context(tc.tile_pool(name="v_packed", bufs=N_HEADS))
+        psum_words = ctx.enter_context(tc.psum_pool(name="psum_words", bufs=2))
+        psum_scores = ctx.enter_context(tc.psum_pool(name="psum_scores", bufs=3))
+        psum_probs = ctx.enter_context(tc.psum_pool(name="psum_probs", bufs=2))
+        psum_out = ctx.enter_context(tc.psum_pool(name="psum_out", bufs=1))
+
+        ident_f32 = consts.tile([P, P], F32)
+        make_identity(nc, ident_f32[:])
+        ident_bf16 = consts.tile([P, P], BF16)
+        make_identity(nc, ident_bf16[:])
+        ones = consts.tile([P, P], BF16)
+        nc.vector.memset(ones[:], 1.0)
+        mask_rows = consts.tile([P, BATCH * SEQ], BF16)
+        nc.vector.memset(mask_rows[:], 0.0)
+        for b in range(BATCH):
+            nc.scalar.dma_start(out=mask_rows[0:1, b * SEQ : (b + 1) * SEQ], in_=attention_mask[b, 0])
+        warm = consts.tile([P, 1], F32)
+        nc.vector.memset(warm[:], 0.0)
+        nc.scalar.activation(out=warm[:], in_=warm[:], func=ACT.Exp)
+
+        k_in, q_in, v_in = [], [], []
+        for g in range(N_HEADS):
+            k_head = inputs.tile([P, PACK * DIM], BF16)
+            nc.sync.dma_start(out=k_head[:], in_=k_rows[g])
+            k_in.append(k_head)
+            q_head = inputs.tile([P, PACK * DIM], BF16)
+            nc.sync.dma_start(out=q_head[:], in_=q_rows[g])
+            q_in.append(q_head)
+            v_head = inputs.tile([P, PACK * DIM], BF16)
+            nc.sync.dma_start(out=v_head[:], in_=v_rows[g])
+            v_in.append(v_head)
+
+        mask_bias = []
+        for b in range(BATCH):
+            mask_ps = psum_scores.tile([P, SEQ], F32, tag="scores_ps")
+            nc.tensor.matmul(
+                out=mask_ps[:], lhsT=ones[:], rhs=mask_rows[:, b * SEQ : (b + 1) * SEQ], start=True, stop=True
+            )
+            bias = consts.tile([P, SEQ], F32, name="mask_bias%d" % b)
+            nc.vector.tensor_scalar(
+                out=bias[:].rearrange("q (j p) -> q j p", j=PACK),
+                in0=mask_ps[:].rearrange("q (p j) -> q j p", j=PACK),
+                scalar1=-NEG_MIN,
+                scalar2=NEG_MIN,
+                op0=ALU.mult,
+                op1=ALU.add,
+            )
+            mask_bias.append(bias)
+
+        words_ps, kT, qT, v_grouped, v_codes, v_scales = {}, {}, {}, {}, {}, {}
+        scores_ps, z, neg_max, expo, row_sum, inv_sum, probs, probsT_ps = {}, {}, {}, {}, {}, {}, {}, {}
+        p_grouped, p_codes, p_scales, out_ps = {}, {}, {}, {}
+
+        def transpose_rows(name, rows_in):
+            words = rows_in[:].bitcast(F32)
+            wordsT_ps = psum_words.tile([P, SEQ], F32)
+            for t in range(PACK):
+                cols = slice(t * P, (t + 1) * P)
+                nc.tensor.transpose(wordsT_ps[:, cols], words[:, cols], ident_f32[:])
+            words_ps[name] = wordsT_ps
+
+        def copy_out_words(name, tag):
+            wordsT = transposed.tile([P, SEQ], F32, name=tag)
+            nc.scalar.copy(out=wordsT[:], in_=words_ps[name][:])
+            return wordsT[:].bitcast(BF16).rearrange("w (c e) -> w e c", e=2)
+
+        def regroup_value(g):
+            grouped = packed.tile([P, DIM, PACK], BF16, name="v_grouped", align_bytes=64)
+            nc.vector.tensor_copy(
+                out=grouped[:].rearrange("p (c i) j -> p c j i", i=4),
+                in_=v_in[g][:].rearrange("p (j c i) -> p c j i", j=PACK, i=4),
+            )
+            v_grouped[g] = grouped
+
+        def quantise_value(g):
+            codes = v_packed.tile([P, DIM], U32, name="v_codes", align_bytes=64)
+            scales = v_packed.tile([P, DIM], U8, name="v_scales", align_bytes=64)
+            nc.vector.quantize_mx(
+                out=codes[:].bitcast(FP8X4), scales=scales[:], in_=v_grouped[g][:].rearrange("p d j -> p (d j)")
+            )
+            v_codes[g], v_scales[g] = codes, scales
+
+        def scores(i):
+            g, t = divmod(i, Q_TILES)
+            acc = psum_scores.tile([P, SEQ], F32, name="scores_ps")
+            for parity in range(2):
+                nc.tensor.matmul(
+                    out=acc[:],
+                    lhsT=qT[g][:, parity, t * P : (t + 1) * P],
+                    rhs=kT[g][:, parity, :],
+                    start=(parity == 0),
+                    stop=(parity == 1),
+                )
+            scores_ps[i] = acc
+
+        def mask_scores(i):
+            masked = work.tile([P, SEQ], F32, name="z")
+            nc.vector.scalar_tensor_tensor(
+                out=masked[:],
+                in0=scores_ps[i][:],
+                scalar=SCALE,
+                in1=mask_bias[i // (HEADS * Q_TILES)][:],
+                op0=ALU.mult,
+                op1=ALU.add,
+            )
+            z[i] = masked
+
+        def row_max(i):
+            negated = stats.tile([P, 1], F32, name="neg_max")
+            nc.vector.tensor_reduce(out=negated[:], in_=z[i][:], axis=AXIS.X, op=ALU.max, negate=True)
+            neg_max[i] = negated
+
+        def exponentials(i):
+            e_tile = work.tile([P, SEQ], F32, name="expo")
+            total = stats.tile([P, 1], F32, name="row_sum")
+            nc.scalar.activation(
+                out=e_tile[:], in_=z[i][:], func=ACT.Exp, bias=neg_max[i][:], scale=1.0, accum_out=total[:]
+            )
+            expo[i], row_sum[i] = e_tile, total
+
+        def invert_sum(i):
+            inverse = stats.tile([P, 1], F32, name="inv_sum")
+            nc.vector.reciprocal(out=inverse[:], in_=row_sum[i][:])
+            inv_sum[i] = inverse
+
+        def normalise(i):
+            p_tile = work.tile([P, SEQ], BF16, name="probs")
+            nc.vector.tensor_scalar(out=p_tile[:], in0=expo[i][:], scalar1=inv_sum[i][:], scalar2=None, op0=ALU.mult)
+            probs[i] = p_tile
+
+        def transpose_probs(i):
+            pT = psum_probs.tile([P, PACK, P], BF16, name="probsT_ps")
+            for j in range(PACK):
+                nc.tensor.transpose(pT[:, j, :], probs[i][:, j * P : (j + 1) * P], ident_bf16[:])
+            probsT_ps[i] = pT
+
+        def group_probs(i):
+            pair, half = divmod(i, 2)
+            if half == 0:
+                p_grouped[pair] = packed.tile([P, 2, P, PACK], BF16, name="p_grouped", align_bytes=64)
+            nc.scalar.copy(out=p_grouped[pair][:, half], in_=probsT_ps[i][:].rearrange("p j q -> p q j"))
+
+        def quantise_probs(pair):
+            codes = packed.tile([P, 2 * P], U32, name="p_codes", align_bytes=64)
+            scales = packed.tile([P, 2 * P], U8, name="p_scales", align_bytes=64)
+            nc.vector.quantize_mx(
+                out=codes[:].bitcast(FP8X4), scales=scales[:], in_=p_grouped[pair][:].rearrange("p a q j -> p (a q j)")
+            )
+            p_codes[pair], p_scales[pair] = codes, scales
+
+        def attend(pair):
+            g = pair // 2
+            acc = psum_out.tile([P, 2, DIM], F32, name="out_ps")
+            for half in range(2):
+                cols = slice(half * P, (half + 1) * P)
+                nc.tensor.matmul_mx(
+                    out=acc[:, half, :],
+                    lhsT=p_codes[pair][:, cols].bitcast(FP8X4),
+                    lhsT_scale=p_scales[pair][:, cols],
+                    rhs=v_codes[g][:].bitcast(FP8X4),
+                    rhs_scale=v_scales[g][:],
+                    start=True,
+                    stop=True,
+                )
+            out_ps[pair] = acc
+
+        def store(pair):
+            g, t_pair = divmod(pair, 2)
+            result = work.tile([P, 2, DIM], F32, name="out_sb")
+            nc.scalar.copy(out=result[:], in_=out_ps[pair][:])
+            nc.sync.dma_start(out=out_rows[g][:, 2 * t_pair : 2 * t_pair + 2, :], in_=result[:])
+
+        def is_tile(i):
+            return 0 <= i < N_TILES
+
+        def pair_ending_at(i):
+            return i // 2 if is_tile(i) and i % 2 == 1 else None
+
+        for step in range(-PREP_STEPS, N_TILES + DRAIN_STEPS):
+            g, phase = divmod(step + PREP_STEPS, Q_TILES)
+            preparing = g < N_HEADS
+
+            if preparing and phase == 0:
+                transpose_rows("k", k_in[g])
+            if preparing and phase == 2:
+                transpose_rows("q", q_in[g])
+            if is_tile(step - 4):
+                transpose_probs(step - 4)
+            if is_tile(step):
+                scores(step)
+            if pair_ending_at(step - 7) is not None:
+                attend(pair_ending_at(step - 7))
+
+            if is_tile(step - 3):
+                invert_sum(step - 3)
+            if is_tile(step - 1):
+                mask_scores(step - 1)
+            if is_tile(step - 3):
+                normalise(step - 3)
+            if is_tile(step - 1):
+                row_max(step - 1)
+            if pair_ending_at(step - 6) is not None:
+                quantise_probs(pair_ending_at(step - 6))
+            if preparing and phase == 1:
+                regroup_value(g)
+            if preparing and phase == 3:
+                quantise_value(g)
+
+            if is_tile(step - 2):
+                exponentials(step - 2)
+            if is_tile(step - 5):
+                group_probs(step - 5)
+            if preparing and phase == 1:
+                kT[g] = copy_out_words("k", "kT")
+            if preparing and phase == 3:
+                qT[g] = copy_out_words("q", "qT")
+            if pair_ending_at(step - 8) is not None:
+                store(pair_ending_at(step - 8))

@@ -25,7 +25,15 @@ NEG_MIN = -3.4028234663852886e38
 FLOPS = 2 * (2 * N_HEADS * SEQ * SEQ * DIM)
 
 PREP_STEPS = 5
-DRAIN_STEPS = 8
+LAG_MASK = 1
+LAG_MAX = 2
+LAG_EXP = 3
+LAG_NORMALISE = 4
+LAG_TRANSPOSE = 6
+LAG_GROUP = 7
+LAG_QUANTISE = 8
+LAG_ATTEND = 9
+LAG_STORE = 10
 
 
 def tile_scaleddotproductattention_t_kernel(tc, query, key, value, attention_mask, out):
@@ -41,8 +49,8 @@ def tile_scaleddotproductattention_t_kernel(tc, query, key, value, attention_mas
         consts = ctx.enter_context(tc.tile_pool(name="consts", bufs=1))
         inputs = ctx.enter_context(tc.tile_pool(name="inputs", bufs=N_HEADS))
         transposed = ctx.enter_context(tc.tile_pool(name="transposed", bufs=2))
-        work = ctx.enter_context(tc.tile_pool(name="work", bufs=3))
-        stats = ctx.enter_context(tc.tile_pool(name="stats", bufs=3))
+        work = ctx.enter_context(tc.tile_pool(name="work", bufs=4))
+        stats = ctx.enter_context(tc.tile_pool(name="stats", bufs=4))
         packed = ctx.enter_context(tc.tile_pool(name="packed", bufs=2))
         v_packed = ctx.enter_context(tc.tile_pool(name="v_packed", bufs=N_HEADS))
         psum_words = ctx.enter_context(tc.psum_pool(name="psum_words", bufs=2))
@@ -77,7 +85,8 @@ def tile_scaleddotproductattention_t_kernel(tc, query, key, value, attention_mas
             v_in.append(v_head)
 
         mask_bias = []
-        for b in range(BATCH):
+
+        def spread_mask(b):
             mask_ps = psum_scores.tile([P, SEQ], F32, tag="scores_ps")
             nc.tensor.matmul(
                 out=mask_ps[:], lhsT=ones[:], rhs=mask_rows[:, b * SEQ : (b + 1) * SEQ], start=True, stop=True
@@ -105,10 +114,18 @@ def tile_scaleddotproductattention_t_kernel(tc, query, key, value, attention_mas
                 nc.tensor.transpose(wordsT_ps[:, cols], words[:, cols], ident_f32[:])
             words_ps[name] = wordsT_ps
 
-        def copy_out_words(name, tag):
-            wordsT = transposed.tile([P, SEQ], F32, name=tag)
-            nc.scalar.copy(out=wordsT[:], in_=words_ps[name][:])
+        def by_parity(wordsT):
             return wordsT[:].bitcast(BF16).rearrange("w (c e) -> w e c", e=2)
+
+        def copy_out_key_words(g):
+            wordsT = transposed.tile([P, SEQ], F32, name="kT")
+            nc.scalar.copy(out=wordsT[:], in_=words_ps["k"][:])
+            kT[g] = by_parity(wordsT)
+
+        def copy_out_query_words(g):
+            wordsT = transposed.tile([P, SEQ], F32, name="qT")
+            nc.vector.tensor_copy(out=wordsT[:], in_=words_ps["q"][:])
+            qT[g] = by_parity(wordsT)
 
         def regroup_value(g):
             grouped = packed.tile([P, DIM, PACK], BF16, name="v_grouped", align_bytes=64)
@@ -171,7 +188,9 @@ def tile_scaleddotproductattention_t_kernel(tc, query, key, value, attention_mas
 
         def normalise(i):
             p_tile = work.tile([P, SEQ], BF16, name="probs")
-            nc.vector.tensor_scalar(out=p_tile[:], in0=expo[i][:], scalar1=inv_sum[i][:], scalar2=None, op0=ALU.mult)
+            nc.gpsimd.tensor_scalar(
+                out=p_tile[:], in0=expo[i][:], scalar1=inv_sum[i][:], scalar2=0.0, op0=ALU.mult, op1=ALU.add
+            )
             probs[i] = p_tile
 
         def transpose_probs(i):
@@ -222,7 +241,7 @@ def tile_scaleddotproductattention_t_kernel(tc, query, key, value, attention_mas
         def pair_ending_at(i):
             return i // 2 if is_tile(i) and i % 2 == 1 else None
 
-        for step in range(-PREP_STEPS, N_TILES + DRAIN_STEPS):
+        def pipeline_step(step):
             g, phase = divmod(step + PREP_STEPS, Q_TILES)
             preparing = g < N_HEADS
 
@@ -230,35 +249,43 @@ def tile_scaleddotproductattention_t_kernel(tc, query, key, value, attention_mas
                 transpose_rows("k", k_in[g])
             if preparing and phase == 2:
                 transpose_rows("q", q_in[g])
-            if is_tile(step - 4):
-                transpose_probs(step - 4)
+            if is_tile(step - LAG_TRANSPOSE):
+                transpose_probs(step - LAG_TRANSPOSE)
             if is_tile(step):
                 scores(step)
-            if pair_ending_at(step - 7) is not None:
-                attend(pair_ending_at(step - 7))
+            if pair_ending_at(step - LAG_ATTEND) is not None:
+                attend(pair_ending_at(step - LAG_ATTEND))
 
-            if is_tile(step - 3):
-                invert_sum(step - 3)
-            if is_tile(step - 1):
-                mask_scores(step - 1)
-            if is_tile(step - 3):
-                normalise(step - 3)
-            if is_tile(step - 1):
-                row_max(step - 1)
-            if pair_ending_at(step - 6) is not None:
-                quantise_probs(pair_ending_at(step - 6))
+            if pair_ending_at(step - LAG_QUANTISE) is not None:
+                quantise_probs(pair_ending_at(step - LAG_QUANTISE))
             if preparing and phase == 1:
                 regroup_value(g)
             if preparing and phase == 3:
                 quantise_value(g)
-
-            if is_tile(step - 2):
-                exponentials(step - 2)
-            if is_tile(step - 5):
-                group_probs(step - 5)
-            if preparing and phase == 1:
-                kT[g] = copy_out_words("k", "kT")
+            if is_tile(step - LAG_NORMALISE):
+                invert_sum(step - LAG_NORMALISE)
+            if is_tile(step - LAG_MASK):
+                mask_scores(step - LAG_MASK)
+            if is_tile(step - LAG_MAX):
+                row_max(step - LAG_MAX)
             if preparing and phase == 3:
-                qT[g] = copy_out_words("q", "qT")
-            if pair_ending_at(step - 8) is not None:
-                store(pair_ending_at(step - 8))
+                copy_out_query_words(g)
+
+            if is_tile(step - LAG_NORMALISE):
+                normalise(step - LAG_NORMALISE)
+
+            if is_tile(step - LAG_EXP):
+                exponentials(step - LAG_EXP)
+            if is_tile(step - LAG_GROUP):
+                group_probs(step - LAG_GROUP)
+            if preparing and phase == 1:
+                copy_out_key_words(g)
+            if pair_ending_at(step - LAG_STORE) is not None:
+                store(pair_ending_at(step - LAG_STORE))
+
+        for step in range(-PREP_STEPS, 0):
+            pipeline_step(step)
+        for b in range(BATCH):
+            spread_mask(b)
+        for step in range(0, N_TILES + LAG_STORE):
+            pipeline_step(step)

@@ -18,22 +18,20 @@ BATCH, HEADS, SEQ, DIM = 2, 4, 512, 256
 N_HEADS = BATCH * HEADS
 Q_TILES = SEQ // P
 N_TILES = N_HEADS * Q_TILES
-N_PAIRS = N_TILES // 2
 SCALE = 1.0 / 16.0
 NEG_MIN = -3.4028234663852886e38
 
 FLOPS = 2 * (2 * N_HEADS * SEQ * SEQ * DIM)
 
-PREP_STEPS = 5
-LAG_MASK = 1
-LAG_MAX = 2
-LAG_EXP = 3
-LAG_NORMALISE = 4
-LAG_TRANSPOSE = 6
-LAG_GROUP = 7
-LAG_QUANTISE = 8
-LAG_ATTEND = 9
-LAG_STORE = 10
+PREP_STEPS = 6
+LAG_MAX = 1
+LAG_EXP = 2
+LAG_NORMALISE = 3
+LAG_TRANSPOSE = 5
+LAG_GROUP = 6
+LAG_QUANTISE = 7
+LAG_ATTEND = 8
+LAG_STORE = 9
 
 
 def tile_scaleddotproductattention_t_kernel(tc, query, key, value, attention_mask, out):
@@ -43,6 +41,7 @@ def tile_scaleddotproductattention_t_kernel(tc, query, key, value, attention_mas
     k_rows = key.rearrange("b h (p j) d -> (b h) p (j d)", j=PACK)
     v_rows = value.rearrange("b h (p j) d -> (b h) p (j d)", j=PACK)
     out_rows = out.rearrange("b h (p t) d -> (b h) p t d", t=PACK)
+    mask_cols = attention_mask.rearrange("b x y (p j) -> p (b x y) j", j=PACK)
 
     with ExitStack() as ctx:
         ctx.enter_context(tc.manual_schedule())
@@ -53,8 +52,8 @@ def tile_scaleddotproductattention_t_kernel(tc, query, key, value, attention_mas
         stats = ctx.enter_context(tc.tile_pool(name="stats", bufs=4))
         packed = ctx.enter_context(tc.tile_pool(name="packed", bufs=2))
         v_packed = ctx.enter_context(tc.tile_pool(name="v_packed", bufs=N_HEADS))
-        psum_words = ctx.enter_context(tc.psum_pool(name="psum_words", bufs=2))
-        psum_scores = ctx.enter_context(tc.psum_pool(name="psum_scores", bufs=3))
+        psum_words = ctx.enter_context(tc.psum_pool(name="psum_words", bufs=1))
+        psum_scores = ctx.enter_context(tc.psum_pool(name="psum_scores", bufs=4))
         psum_probs = ctx.enter_context(tc.psum_pool(name="psum_probs", bufs=2))
         psum_out = ctx.enter_context(tc.psum_pool(name="psum_out", bufs=1))
 
@@ -62,12 +61,9 @@ def tile_scaleddotproductattention_t_kernel(tc, query, key, value, attention_mas
         make_identity(nc, ident_f32[:])
         ident_bf16 = consts.tile([P, P], BF16)
         make_identity(nc, ident_bf16[:])
-        ones = consts.tile([P, P], BF16)
-        nc.vector.memset(ones[:], 1.0)
-        mask_rows = consts.tile([P, BATCH * SEQ], BF16)
-        nc.vector.memset(mask_rows[:], 0.0)
-        for b in range(BATCH):
-            nc.scalar.dma_start(out=mask_rows[0:1, b * SEQ : (b + 1) * SEQ], in_=attention_mask[b, 0])
+        mask_in = consts.tile([P, BATCH, PACK], BF16)
+        with nc.allow_non_contiguous_dma(reason="1 KiB of mask, 8 bytes to a partition"):
+            nc.scalar.dma_start(out=mask_in[:], in_=mask_cols)
         warm = consts.tile([P, 1], F32)
         nc.vector.memset(warm[:], 0.0)
         nc.scalar.activation(out=warm[:], in_=warm[:], func=ACT.Exp)
@@ -84,26 +80,15 @@ def tile_scaleddotproductattention_t_kernel(tc, query, key, value, attention_mas
             nc.sync.dma_start(out=v_head[:], in_=v_rows[g])
             v_in.append(v_head)
 
-        mask_bias = []
-
-        def spread_mask(b):
-            mask_ps = psum_scores.tile([P, SEQ], F32, tag="scores_ps")
-            nc.tensor.matmul(
-                out=mask_ps[:], lhsT=ones[:], rhs=mask_rows[:, b * SEQ : (b + 1) * SEQ], start=True, stop=True
-            )
-            bias = consts.tile([P, SEQ], F32, name="mask_bias%d" % b)
-            nc.vector.tensor_scalar(
-                out=bias[:].rearrange("q (j p) -> q j p", j=PACK),
-                in0=mask_ps[:].rearrange("q (p j) -> q j p", j=PACK),
-                scalar1=-NEG_MIN,
-                scalar2=NEG_MIN,
-                op0=ALU.mult,
-                op1=ALU.add,
-            )
-            mask_bias.append(bias)
+        mask_term = consts.tile([P, BATCH, PACK], F32)
+        nc.vector.tensor_scalar(
+            out=mask_term[:], in0=mask_in[:], scalar1=-NEG_MIN, scalar2=NEG_MIN, op0=ALU.mult, op1=ALU.add
+        )
+        mask_termT = consts.tile([P, BATCH, PACK, P], F32)
+        nc.vector.tensor_copy(out=mask_termT[:], in_=mask_term[:].unsqueeze(3).to_broadcast([P, BATCH, PACK, P]))
 
         words_ps, kT, qT, v_grouped, v_codes, v_scales = {}, {}, {}, {}, {}, {}
-        scores_ps, z, neg_max, expo, row_sum, inv_sum, probs, probsT_ps = {}, {}, {}, {}, {}, {}, {}, {}
+        z_ps, neg_max, expo, row_sum, inv_sum, probs, probsT_ps = {}, {}, {}, {}, {}, {}, {}
         p_grouped, p_codes, p_scales, out_ps = {}, {}, {}, {}
 
         def transpose_rows(name, rows_in):
@@ -114,18 +99,20 @@ def tile_scaleddotproductattention_t_kernel(tc, query, key, value, attention_mas
                 nc.tensor.transpose(wordsT_ps[:, cols], words[:, cols], ident_f32[:])
             words_ps[name] = wordsT_ps
 
-        def by_parity(wordsT):
-            return wordsT[:].bitcast(BF16).rearrange("w (c e) -> w e c", e=2)
+        def by_parity(pairs):
+            return pairs.rearrange("w (c e) -> w e c", e=2)
 
         def copy_out_key_words(g):
             wordsT = transposed.tile([P, SEQ], F32, name="kT")
             nc.scalar.copy(out=wordsT[:], in_=words_ps["k"][:])
-            kT[g] = by_parity(wordsT)
+            kT[g] = by_parity(wordsT[:].bitcast(BF16))
 
-        def copy_out_query_words(g):
-            wordsT = transposed.tile([P, SEQ], F32, name="qT")
-            nc.vector.tensor_copy(out=wordsT[:], in_=words_ps["q"][:])
-            qT[g] = by_parity(wordsT)
+        def copy_out_scaled_query(g):
+            scaled = transposed.tile([P, 2 * SEQ], BF16, name="qT")
+            nc.vector.tensor_scalar(
+                out=scaled[:], in0=words_ps["q"][:].bitcast(BF16), scalar1=SCALE, scalar2=None, op0=ALU.mult
+            )
+            qT[g] = by_parity(scaled[:])
 
         def regroup_value(g):
             grouped = packed.tile([P, DIM, PACK], BF16, name="v_grouped", align_bytes=64)
@@ -143,41 +130,38 @@ def tile_scaleddotproductattention_t_kernel(tc, query, key, value, attention_mas
             )
             v_codes[g], v_scales[g] = codes, scales
 
-        def scores(i):
+        def masked_scores(i):
             g, t = divmod(i, Q_TILES)
-            acc = psum_scores.tile([P, SEQ], F32, name="scores_ps")
+            acc = psum_scores.tile([P, SEQ], F32, name="z_ps")
+            for j in range(PACK):
+                nc.tensor.matmul(
+                    out=acc[:, j * P : (j + 1) * P],
+                    lhsT=mask_termT[:, g // HEADS, j, :],
+                    rhs=ident_f32[:],
+                    is_transpose=True,
+                    start=(j == 0),
+                    stop=False,
+                )
             for parity in range(2):
                 nc.tensor.matmul(
                     out=acc[:],
                     lhsT=qT[g][:, parity, t * P : (t + 1) * P],
                     rhs=kT[g][:, parity, :],
-                    start=(parity == 0),
+                    start=False,
                     stop=(parity == 1),
                 )
-            scores_ps[i] = acc
-
-        def mask_scores(i):
-            masked = work.tile([P, SEQ], F32, name="z")
-            nc.vector.scalar_tensor_tensor(
-                out=masked[:],
-                in0=scores_ps[i][:],
-                scalar=SCALE,
-                in1=mask_bias[i // (HEADS * Q_TILES)][:],
-                op0=ALU.mult,
-                op1=ALU.add,
-            )
-            z[i] = masked
+            z_ps[i] = acc
 
         def row_max(i):
             negated = stats.tile([P, 1], F32, name="neg_max")
-            nc.vector.tensor_reduce(out=negated[:], in_=z[i][:], axis=AXIS.X, op=ALU.max, negate=True)
+            nc.vector.tensor_reduce(out=negated[:], in_=z_ps[i][:], axis=AXIS.X, op=ALU.max, negate=True)
             neg_max[i] = negated
 
         def exponentials(i):
             e_tile = work.tile([P, SEQ], F32, name="expo")
             total = stats.tile([P, 1], F32, name="row_sum")
             nc.scalar.activation(
-                out=e_tile[:], in_=z[i][:], func=ACT.Exp, bias=neg_max[i][:], scale=1.0, accum_out=total[:]
+                out=e_tile[:], in_=z_ps[i][:], func=ACT.Exp, bias=neg_max[i][:], scale=1.0, accum_out=total[:]
             )
             expo[i], row_sum[i] = e_tile, total
 
@@ -232,7 +216,7 @@ def tile_scaleddotproductattention_t_kernel(tc, query, key, value, attention_mas
         def store(pair):
             g, t_pair = divmod(pair, 2)
             result = work.tile([P, 2, DIM], F32, name="out_sb")
-            nc.scalar.copy(out=result[:], in_=out_ps[pair][:])
+            nc.vector.tensor_copy(out=result[:], in_=out_ps[pair][:])
             nc.sync.dma_start(out=out_rows[g][:, 2 * t_pair : 2 * t_pair + 2, :], in_=result[:])
 
         def is_tile(i):
@@ -241,10 +225,12 @@ def tile_scaleddotproductattention_t_kernel(tc, query, key, value, attention_mas
         def pair_ending_at(i):
             return i // 2 if is_tile(i) and i % 2 == 1 else None
 
-        def pipeline_step(step):
+        for step in range(-PREP_STEPS, N_TILES + LAG_STORE):
             g, phase = divmod(step + PREP_STEPS, Q_TILES)
             preparing = g < N_HEADS
 
+            if pair_ending_at(step - LAG_ATTEND) is not None:
+                attend(pair_ending_at(step - LAG_ATTEND))
             if preparing and phase == 0:
                 transpose_rows("k", k_in[g])
             if preparing and phase == 2:
@@ -252,9 +238,7 @@ def tile_scaleddotproductattention_t_kernel(tc, query, key, value, attention_mas
             if is_tile(step - LAG_TRANSPOSE):
                 transpose_probs(step - LAG_TRANSPOSE)
             if is_tile(step):
-                scores(step)
-            if pair_ending_at(step - LAG_ATTEND) is not None:
-                attend(pair_ending_at(step - LAG_ATTEND))
+                masked_scores(step)
 
             if pair_ending_at(step - LAG_QUANTISE) is not None:
                 quantise_probs(pair_ending_at(step - LAG_QUANTISE))
@@ -264,12 +248,12 @@ def tile_scaleddotproductattention_t_kernel(tc, query, key, value, attention_mas
                 quantise_value(g)
             if is_tile(step - LAG_NORMALISE):
                 invert_sum(step - LAG_NORMALISE)
-            if is_tile(step - LAG_MASK):
-                mask_scores(step - LAG_MASK)
             if is_tile(step - LAG_MAX):
                 row_max(step - LAG_MAX)
             if preparing and phase == 3:
-                copy_out_query_words(g)
+                copy_out_scaled_query(g)
+            if pair_ending_at(step - LAG_STORE) is not None:
+                store(pair_ending_at(step - LAG_STORE))
 
             if is_tile(step - LAG_NORMALISE):
                 normalise(step - LAG_NORMALISE)
@@ -280,12 +264,3 @@ def tile_scaleddotproductattention_t_kernel(tc, query, key, value, attention_mas
                 group_probs(step - LAG_GROUP)
             if preparing and phase == 1:
                 copy_out_key_words(g)
-            if pair_ending_at(step - LAG_STORE) is not None:
-                store(pair_ending_at(step - LAG_STORE))
-
-        for step in range(-PREP_STEPS, 0):
-            pipeline_step(step)
-        for b in range(BATCH):
-            spread_mask(b)
-        for step in range(0, N_TILES + LAG_STORE):
-            pipeline_step(step)

@@ -23,7 +23,7 @@ NEG_MIN = -3.4028234663852886e38
 
 FLOPS = 2 * (2 * N_HEADS * SEQ * SEQ * DIM)
 
-PREP_STEPS = 6
+PREP_STEPS = 4
 LAG_MAX = 1
 LAG_EXP = 2
 LAG_NORMALISE = 3
@@ -130,27 +130,27 @@ def tile_scaleddotproductattention_t_kernel(tc, query, key, value, attention_mas
             )
             v_codes[g], v_scales[g] = codes, scales
 
-        def masked_scores(i):
+        def write_mask_term(i, j):
+            if j == 0:
+                z_ps[i] = psum_scores.tile([P, SEQ], F32, name="z_ps")
+            nc.tensor.matmul(
+                out=z_ps[i][:, j * P : (j + 1) * P],
+                lhsT=mask_termT[:, i // (HEADS * Q_TILES), j, :],
+                rhs=ident_f32[:],
+                is_transpose=True,
+                start=(j == 0),
+                stop=False,
+            )
+
+        def add_scores(i, parity):
             g, t = divmod(i, Q_TILES)
-            acc = psum_scores.tile([P, SEQ], F32, name="z_ps")
-            for j in range(PACK):
-                nc.tensor.matmul(
-                    out=acc[:, j * P : (j + 1) * P],
-                    lhsT=mask_termT[:, g // HEADS, j, :],
-                    rhs=ident_f32[:],
-                    is_transpose=True,
-                    start=(j == 0),
-                    stop=False,
-                )
-            for parity in range(2):
-                nc.tensor.matmul(
-                    out=acc[:],
-                    lhsT=qT[g][:, parity, t * P : (t + 1) * P],
-                    rhs=kT[g][:, parity, :],
-                    start=False,
-                    stop=(parity == 1),
-                )
-            z_ps[i] = acc
+            nc.tensor.matmul(
+                out=z_ps[i][:],
+                lhsT=qT[g][:, parity, t * P : (t + 1) * P],
+                rhs=kT[g][:, parity, :],
+                start=False,
+                stop=(parity == 1),
+            )
 
         def row_max(i):
             negated = stats.tile([P, 1], F32, name="neg_max")
@@ -229,16 +229,20 @@ def tile_scaleddotproductattention_t_kernel(tc, query, key, value, attention_mas
             g, phase = divmod(step + PREP_STEPS, Q_TILES)
             preparing = g < N_HEADS
 
+            if is_tile(step - LAG_TRANSPOSE):
+                transpose_probs(step - LAG_TRANSPOSE)
+            for parity in range(2):
+                if is_tile(step):
+                    add_scores(step, parity)
+                if is_tile(step + 1):
+                    write_mask_term(step + 1, 2 * parity)
+                    write_mask_term(step + 1, 2 * parity + 1)
             if pair_ending_at(step - LAG_ATTEND) is not None:
                 attend(pair_ending_at(step - LAG_ATTEND))
             if preparing and phase == 0:
                 transpose_rows("k", k_in[g])
             if preparing and phase == 2:
                 transpose_rows("q", q_in[g])
-            if is_tile(step - LAG_TRANSPOSE):
-                transpose_probs(step - LAG_TRANSPOSE)
-            if is_tile(step):
-                masked_scores(step)
 
             if pair_ending_at(step - LAG_QUANTISE) is not None:
                 quantise_probs(pair_ending_at(step - LAG_QUANTISE))

@@ -41,7 +41,7 @@ def tile_scaleddotproductattention_t_kernel(tc, query, key, value, attention_mas
     k_rows = key.rearrange("b h (p j) d -> (b h) p (j d)", j=PACK)
     v_rows = value.rearrange("b h (p j) d -> (b h) p (j d)", j=PACK)
     out_rows = out.rearrange("b h (p t) d -> (b h) p t d", t=PACK)
-    mask_cols = attention_mask.rearrange("b x y (p j) -> p (b x y) j", j=PACK)
+    mask_cols = attention_mask.rearrange("b x y (h r u e) -> e r (b x y h) u", h=2, u=2, e=2)
 
     with ExitStack() as ctx:
         ctx.enter_context(tc.manual_schedule())
@@ -59,11 +59,11 @@ def tile_scaleddotproductattention_t_kernel(tc, query, key, value, attention_mas
 
         ident_f32 = consts.tile([P, P], F32)
         make_identity(nc, ident_f32[:])
-        ident_bf16 = consts.tile([P, P], BF16)
-        make_identity(nc, ident_bf16[:])
-        mask_in = consts.tile([P, BATCH, PACK], BF16)
-        with nc.allow_non_contiguous_dma(reason="1 KiB of mask, 8 bytes to a partition"):
-            nc.scalar.dma_start(out=mask_in[:], in_=mask_cols)
+        mask_in = consts.tile([P, 2, BATCH * 2, 4], BF16)
+        with nc.allow_non_contiguous_dma(reason="2 KiB of mask, one value at a time"):
+            for e in range(2):
+                for u in range(2):
+                    nc.scalar.dma_start(out=mask_in[e:P:2, u, :, 0], in_=mask_cols[e, :, :, u])
         warm = consts.tile([P, 1], F32)
         nc.vector.memset(warm[:], 0.0)
         nc.scalar.activation(out=warm[:], in_=warm[:], func=ACT.Exp)
@@ -80,12 +80,12 @@ def tile_scaleddotproductattention_t_kernel(tc, query, key, value, attention_mas
             nc.sync.dma_start(out=v_head[:], in_=v_rows[g])
             v_in.append(v_head)
 
-        mask_term = consts.tile([P, BATCH, PACK], F32)
+        mask_term = consts.tile([P, 2, BATCH * 2], F32)
         nc.vector.tensor_scalar(
-            out=mask_term[:], in0=mask_in[:], scalar1=-NEG_MIN, scalar2=NEG_MIN, op0=ALU.mult, op1=ALU.add
+            out=mask_term[:], in0=mask_in[:, :, :, 0], scalar1=-NEG_MIN, scalar2=NEG_MIN, op0=ALU.mult, op1=ALU.add
         )
-        mask_termT = consts.tile([P, BATCH, PACK, P], F32)
-        nc.vector.tensor_copy(out=mask_termT[:], in_=mask_term[:].unsqueeze(3).to_broadcast([P, BATCH, PACK, P]))
+        mask_termT = consts.tile([P, 2, BATCH * 2, P], F32)
+        nc.vector.tensor_copy(out=mask_termT[:], in_=mask_term[:].unsqueeze(3).to_broadcast([P, 2, BATCH * 2, P]))
 
         words_ps, kT, qT, v_grouped, v_codes, v_scales = {}, {}, {}, {}, {}, {}
         z_ps, neg_max, expo, row_sum, inv_sum, probs, probsT_ps = {}, {}, {}, {}, {}, {}, {}
@@ -104,7 +104,10 @@ def tile_scaleddotproductattention_t_kernel(tc, query, key, value, attention_mas
 
         def copy_out_key_words(g):
             wordsT = transposed.tile([P, SEQ], F32, name="kT")
-            nc.scalar.copy(out=wordsT[:], in_=words_ps["k"][:])
+            nc.scalar.copy(
+                out=wordsT[:].rearrange("w (u p e) -> w u p e", u=2, e=2),
+                in_=words_ps["k"][:].rearrange("w (u e p) -> w u p e", u=2, e=2),
+            )
             kT[g] = by_parity(wordsT[:].bitcast(BF16))
 
         def copy_out_scaled_query(g):
@@ -135,7 +138,7 @@ def tile_scaleddotproductattention_t_kernel(tc, query, key, value, attention_mas
                 z_ps[i] = psum_scores.tile([P, SEQ], F32, name="z_ps")
             nc.tensor.matmul(
                 out=z_ps[i][:, j * P : (j + 1) * P],
-                lhsT=mask_termT[:, i // (HEADS * Q_TILES), j, :],
+                lhsT=mask_termT[:, j // 2, 2 * (i // (HEADS * Q_TILES)) + j % 2, :],
                 rhs=ident_f32[:],
                 is_transpose=True,
                 start=(j == 0),
@@ -178,22 +181,23 @@ def tile_scaleddotproductattention_t_kernel(tc, query, key, value, attention_mas
             probs[i] = p_tile
 
         def transpose_probs(i):
-            pT = psum_probs.tile([P, PACK, P], BF16, name="probsT_ps")
-            for j in range(PACK):
-                nc.tensor.transpose(pT[:, j, :], probs[i][:, j * P : (j + 1) * P], ident_bf16[:])
+            words = probs[i][:].bitcast(F32)
+            pT = psum_probs.tile([P, 2, P], F32, name="probsT_ps")
+            for u in range(2):
+                nc.tensor.transpose(pT[:, u, :], words[:, u * P : (u + 1) * P], ident_f32[:])
             probsT_ps[i] = pT
 
         def group_probs(i):
             pair, half = divmod(i, 2)
             if half == 0:
-                p_grouped[pair] = packed.tile([P, 2, P, PACK], BF16, name="p_grouped", align_bytes=64)
-            nc.scalar.copy(out=p_grouped[pair][:, half], in_=probsT_ps[i][:].rearrange("p j q -> p q j"))
+                p_grouped[pair] = packed.tile([P, 2, P, 2], F32, name="p_grouped", align_bytes=64)
+            nc.scalar.copy(out=p_grouped[pair][:, half], in_=probsT_ps[i][:].rearrange("p u q -> p q u"))
 
         def quantise_probs(pair):
             codes = packed.tile([P, 2 * P], U32, name="p_codes", align_bytes=64)
             scales = packed.tile([P, 2 * P], U8, name="p_scales", align_bytes=64)
             nc.vector.quantize_mx(
-                out=codes[:].bitcast(FP8X4), scales=scales[:], in_=p_grouped[pair][:].rearrange("p a q j -> p (a q j)")
+                out=codes[:].bitcast(FP8X4), scales=scales[:], in_=p_grouped[pair][:].rearrange("p a q u -> p (a q u)").bitcast(BF16)
             )
             p_codes[pair], p_scales[pair] = codes, scales
 
@@ -216,7 +220,7 @@ def tile_scaleddotproductattention_t_kernel(tc, query, key, value, attention_mas
         def store(pair):
             g, t_pair = divmod(pair, 2)
             result = work.tile([P, 2, DIM], F32, name="out_sb")
-            nc.vector.tensor_copy(out=result[:], in_=out_ps[pair][:])
+            nc.scalar.copy(out=result[:], in_=out_ps[pair][:])
             nc.sync.dma_start(out=out_rows[g][:, 2 * t_pair : 2 * t_pair + 2, :], in_=result[:])
 
         def is_tile(i):
@@ -256,8 +260,6 @@ def tile_scaleddotproductattention_t_kernel(tc, query, key, value, attention_mas
                 row_max(step - LAG_MAX)
             if preparing and phase == 3:
                 copy_out_scaled_query(g)
-            if pair_ending_at(step - LAG_STORE) is not None:
-                store(pair_ending_at(step - LAG_STORE))
 
             if is_tile(step - LAG_NORMALISE):
                 normalise(step - LAG_NORMALISE)
@@ -268,3 +270,5 @@ def tile_scaleddotproductattention_t_kernel(tc, query, key, value, attention_mas
                 group_probs(step - LAG_GROUP)
             if preparing and phase == 1:
                 copy_out_key_words(g)
+            if pair_ending_at(step - LAG_STORE) is not None:
+                store(pair_ending_at(step - LAG_STORE))

@@ -63,7 +63,7 @@ def tile_scaleddotproductattention_t_kernel(tc, query, key, value, attention_mas
         with nc.allow_non_contiguous_dma(reason="2 KiB of mask, one value at a time"):
             for e in range(2):
                 for u in range(2):
-                    nc.scalar.dma_start(out=mask_in[e:P:2, u, :, 0], in_=mask_cols[e, :, :, u])
+                    nc.sync.dma_start(out=mask_in[e:P:2, u, :, 0], in_=mask_cols[e, :, :, u])
         warm = consts.tile([P, 1], F32)
         nc.vector.memset(warm[:], 0.0)
         nc.scalar.activation(out=warm[:], in_=warm[:], func=ACT.Exp)
@@ -91,9 +91,9 @@ def tile_scaleddotproductattention_t_kernel(tc, query, key, value, attention_mas
         z_ps, neg_max, expo, row_sum, inv_sum, probs, probsT_ps = {}, {}, {}, {}, {}, {}, {}
         p_grouped, p_codes, p_scales, out_ps = {}, {}, {}, {}
 
-        def transpose_rows(name, rows_in):
+        def transpose_rows(name, rows_in, pool):
             words = rows_in[:].bitcast(F32)
-            wordsT_ps = psum_words.tile([P, SEQ], F32)
+            wordsT_ps = pool.tile([P, SEQ], F32, name="z_ps" if pool is psum_scores else "wordsT_ps")
             for t in range(PACK):
                 cols = slice(t * P, (t + 1) * P)
                 nc.tensor.transpose(wordsT_ps[:, cols], words[:, cols], ident_f32[:])
@@ -244,9 +244,9 @@ def tile_scaleddotproductattention_t_kernel(tc, query, key, value, attention_mas
             if pair_ending_at(step - LAG_ATTEND) is not None:
                 attend(pair_ending_at(step - LAG_ATTEND))
             if preparing and phase == 0:
-                transpose_rows("k", k_in[g])
+                transpose_rows("k", k_in[g], psum_words)
             if preparing and phase == 2:
-                transpose_rows("q", q_in[g])
+                transpose_rows("q", q_in[g], psum_scores if g == 0 else psum_words)
 
             if pair_ending_at(step - LAG_QUANTISE) is not None:
                 quantise_probs(pair_ending_at(step - LAG_QUANTISE))

@@ -41,7 +41,7 @@ def tile_scaleddotproductattention_t_kernel(tc, query, key, value, attention_mas
     k_rows = key.rearrange("b h (p j) d -> (b h) p (j d)", j=PACK)
     v_rows = value.rearrange("b h (p j) d -> (b h) p (j d)", j=PACK)
     out_rows = out.rearrange("b h (p t) d -> (b h) p t d", t=PACK)
-    mask_cols = attention_mask.rearrange("b x y (h r u e) -> e r (b x y h) u", h=2, u=2, e=2)
+    mask_cols = attention_mask.rearrange("b x y (h c u) -> c (b x y h) u", h=2, u=2)
 
     with ExitStack() as ctx:
         ctx.enter_context(tc.manual_schedule())
@@ -59,11 +59,9 @@ def tile_scaleddotproductattention_t_kernel(tc, query, key, value, attention_mas
 
         ident_f32 = consts.tile([P, P], F32)
         make_identity(nc, ident_f32[:])
-        mask_in = consts.tile([P, 2, BATCH * 2, 4], BF16)
-        with nc.allow_non_contiguous_dma(reason="2 KiB of mask, one value at a time"):
-            for e in range(2):
-                for u in range(2):
-                    nc.sync.dma_start(out=mask_in[e:P:2, u, :, 0], in_=mask_cols[e, :, :, u])
+        mask_in = consts.tile([P, BATCH * 2, 2], BF16)
+        with nc.allow_non_contiguous_dma(reason="2 KiB of mask, 4 bytes at a time"):
+            nc.scalar.dma_start(out=mask_in[:], in_=mask_cols)
         warm = consts.tile([P, 1], F32)
         nc.vector.memset(warm[:], 0.0)
         nc.scalar.activation(out=warm[:], in_=warm[:], func=ACT.Exp)
@@ -80,12 +78,18 @@ def tile_scaleddotproductattention_t_kernel(tc, query, key, value, attention_mas
             nc.sync.dma_start(out=v_head[:], in_=v_rows[g])
             v_in.append(v_head)
 
-        mask_term = consts.tile([P, 2, BATCH * 2], F32)
+        mask_term = consts.tile([P, BATCH * 2, 2], F32)
         nc.vector.tensor_scalar(
-            out=mask_term[:], in0=mask_in[:, :, :, 0], scalar1=-NEG_MIN, scalar2=NEG_MIN, op0=ALU.mult, op1=ALU.add
+            out=mask_term[:], in0=mask_in[:], scalar1=-NEG_MIN, scalar2=NEG_MIN, op0=ALU.mult, op1=ALU.add
         )
-        mask_termT = consts.tile([P, 2, BATCH * 2, P], F32)
-        nc.vector.tensor_copy(out=mask_termT[:], in_=mask_term[:].unsqueeze(3).to_broadcast([P, 2, BATCH * 2, P]))
+        mask_termT = consts.tile([P, BATCH * 2, 2, P], F32)
+        nc.vector.tensor_copy(out=mask_termT[:], in_=mask_term[:].unsqueeze(3).to_broadcast([P, BATCH * 2, 2, P]))
+
+        batches = [[i, i + 1] for i in range(0, N_TILES - 2, 2)] + [[N_TILES - 2], [N_TILES - 1]]
+        batch_of = {}
+        for n, tiles in enumerate(batches):
+            for i in tiles:
+                batch_of[i] = n
 
         words_ps, kT, qT, v_grouped, v_codes, v_scales = {}, {}, {}, {}, {}, {}
         z_ps, neg_max, expo, row_sum, inv_sum, probs, probsT_ps = {}, {}, {}, {}, {}, {}, {}
@@ -106,7 +110,7 @@ def tile_scaleddotproductattention_t_kernel(tc, query, key, value, attention_mas
             wordsT = transposed.tile([P, SEQ], F32, name="kT")
             nc.scalar.copy(
                 out=wordsT[:].rearrange("w (u p e) -> w u p e", u=2, e=2),
-                in_=words_ps["k"][:].rearrange("w (u e p) -> w u p e", u=2, e=2),
+                in_=words_ps["k"][:].rearrange("w (e u p) -> w u p e", u=2, e=2),
             )
             kT[g] = by_parity(wordsT[:].bitcast(BF16))
 
@@ -120,8 +124,8 @@ def tile_scaleddotproductattention_t_kernel(tc, query, key, value, attention_mas
         def regroup_value(g):
             grouped = packed.tile([P, DIM, PACK], BF16, name="v_grouped", align_bytes=64)
             nc.vector.tensor_copy(
-                out=grouped[:].rearrange("p (c i) j -> p c j i", i=4),
-                in_=v_in[g][:].rearrange("p (j c i) -> p c j i", j=PACK, i=4),
+                out=grouped[:].rearrange("p d (u e) -> p d u e", u=2),
+                in_=v_in[g][:].rearrange("p (e u d) -> p d u e", e=2, u=2),
             )
             v_grouped[g] = grouped
 
@@ -138,7 +142,7 @@ def tile_scaleddotproductattention_t_kernel(tc, query, key, value, attention_mas
                 z_ps[i] = psum_scores.tile([P, SEQ], F32, name="z_ps")
             nc.tensor.matmul(
                 out=z_ps[i][:, j * P : (j + 1) * P],
-                lhsT=mask_termT[:, j // 2, 2 * (i // (HEADS * Q_TILES)) + j % 2, :],
+                lhsT=mask_termT[:, 2 * (i // (HEADS * Q_TILES)) + j % 2, j // 2, :],
                 rhs=ident_f32[:],
                 is_transpose=True,
                 start=(j == 0),
@@ -175,9 +179,12 @@ def tile_scaleddotproductattention_t_kernel(tc, query, key, value, attention_mas
 
         def normalise(i):
             p_tile = work.tile([P, SEQ], BF16, name="probs")
-            nc.gpsimd.tensor_scalar(
-                out=p_tile[:], in0=expo[i][:], scalar1=inv_sum[i][:], scalar2=0.0, op0=ALU.mult, op1=ALU.add
-            )
+            if len(batches[batch_of[i]]) == 1:
+                nc.vector.tensor_scalar(out=p_tile[:], in0=expo[i][:], scalar1=inv_sum[i][:], scalar2=None, op0=ALU.mult)
+            else:
+                nc.gpsimd.tensor_scalar(
+                    out=p_tile[:], in0=expo[i][:], scalar1=inv_sum[i][:], scalar2=0.0, op0=ALU.mult, op1=ALU.add
+                )
             probs[i] = p_tile
 
         def transpose_probs(i):
@@ -188,46 +195,50 @@ def tile_scaleddotproductattention_t_kernel(tc, query, key, value, attention_mas
             probsT_ps[i] = pT
 
         def group_probs(i):
-            pair, half = divmod(i, 2)
-            if half == 0:
-                p_grouped[pair] = packed.tile([P, 2, P, 2], F32, name="p_grouped", align_bytes=64)
-            nc.scalar.copy(out=p_grouped[pair][:, half], in_=probsT_ps[i][:].rearrange("p u q -> p q u"))
+            n = batch_of[i]
+            place = batches[n].index(i)
+            if place == 0:
+                p_grouped[n] = packed.tile([P, len(batches[n]), P, 2], F32, name="p_grouped", align_bytes=64)
+            nc.scalar.copy(out=p_grouped[n][:, place], in_=probsT_ps[i][:].rearrange("p u q -> p q u"))
 
-        def quantise_probs(pair):
-            codes = packed.tile([P, 2 * P], U32, name="p_codes", align_bytes=64)
-            scales = packed.tile([P, 2 * P], U8, name="p_scales", align_bytes=64)
+        def quantise_probs(n):
+            codes = packed.tile([P, len(batches[n]) * P], U32, name="p_codes", align_bytes=64)
+            scales = packed.tile([P, len(batches[n]) * P], U8, name="p_scales", align_bytes=64)
             nc.vector.quantize_mx(
-                out=codes[:].bitcast(FP8X4), scales=scales[:], in_=p_grouped[pair][:].rearrange("p a q u -> p (a q u)").bitcast(BF16)
+                out=codes[:].bitcast(FP8X4), scales=scales[:], in_=p_grouped[n][:].rearrange("p a q u -> p (a q u)").bitcast(BF16)
             )
-            p_codes[pair], p_scales[pair] = codes, scales
+            p_codes[n], p_scales[n] = codes, scales
 
-        def attend(pair):
-            g = pair // 2
-            acc = psum_out.tile([P, 2, DIM], F32, name="out_ps")
-            for half in range(2):
-                cols = slice(half * P, (half + 1) * P)
+        def attend(n):
+            g = batches[n][0] // Q_TILES
+            if n == len(batches) - 1:
+                acc = psum_words.tile([P, len(batches[n]), DIM], F32, name="wordsT_ps")
+            else:
+                acc = psum_out.tile([P, len(batches[n]), DIM], F32, name="out_ps")
+            for place in range(len(batches[n])):
+                cols = slice(place * P, (place + 1) * P)
                 nc.tensor.matmul_mx(
-                    out=acc[:, half, :],
-                    lhsT=p_codes[pair][:, cols].bitcast(FP8X4),
-                    lhsT_scale=p_scales[pair][:, cols],
+                    out=acc[:, place, :],
+                    lhsT=p_codes[n][:, cols].bitcast(FP8X4),
+                    lhsT_scale=p_scales[n][:, cols],
                     rhs=v_codes[g][:].bitcast(FP8X4),
                     rhs_scale=v_scales[g][:],
                     start=True,
                     stop=True,
                 )
-            out_ps[pair] = acc
+            out_ps[n] = acc
 
-        def store(pair):
-            g, t_pair = divmod(pair, 2)
-            result = work.tile([P, 2, DIM], F32, name="out_sb")
-            nc.scalar.copy(out=result[:], in_=out_ps[pair][:])
-            nc.sync.dma_start(out=out_rows[g][:, 2 * t_pair : 2 * t_pair + 2, :], in_=result[:])
+        def store(n):
+            g, t = divmod(batches[n][0], Q_TILES)
+            result = work.tile([P, len(batches[n]), DIM], F32, name="out_sb")
+            nc.scalar.copy(out=result[:], in_=out_ps[n][:])
+            nc.sync.dma_start(out=out_rows[g][:, t : t + len(batches[n]), :], in_=result[:])
 
         def is_tile(i):
             return 0 <= i < N_TILES
 
         def pair_ending_at(i):
-            return i // 2 if is_tile(i) and i % 2 == 1 else None
+            return batch_of[i] if is_tile(i) and batches[batch_of[i]][-1] == i else None
 
         for step in range(-PREP_STEPS, N_TILES + LAG_STORE):
             g, phase = divmod(step + PREP_STEPS, Q_TILES)
@@ -235,14 +246,15 @@ def tile_scaleddotproductattention_t_kernel(tc, query, key, value, attention_mas
 
             if is_tile(step - LAG_TRANSPOSE):
                 transpose_probs(step - LAG_TRANSPOSE)
-            for parity in range(2):
-                if is_tile(step):
-                    add_scores(step, parity)
-                if is_tile(step + 1):
-                    write_mask_term(step + 1, 2 * parity)
-                    write_mask_term(step + 1, 2 * parity + 1)
+            if is_tile(step):
+                add_scores(step, 0)
             if pair_ending_at(step - LAG_ATTEND) is not None:
                 attend(pair_ending_at(step - LAG_ATTEND))
+            if is_tile(step):
+                add_scores(step, 1)
+            if is_tile(step + 1):
+                for j in range(PACK):
+                    write_mask_term(step + 1, j)
             if preparing and phase == 0:
                 transpose_rows("k", k_in[g], psum_words)
             if preparing and phase == 2:

@@ -23,6 +23,8 @@ NEG_MIN = -3.4028234663852886e38
 
 FLOPS = 2 * (2 * N_HEADS * SEQ * SEQ * DIM)
 
+WARM_PASSES = 4
+
 PREP_STEPS = 4
 LAG_MAX = 1
 LAG_EXP = 2
@@ -65,6 +67,16 @@ def tile_scaleddotproductattention_t_kernel(tc, query, key, value, attention_mas
         warm = consts.tile([P, 1], F32)
         nc.vector.memset(warm[:], 0.0)
         nc.scalar.activation(out=warm[:], in_=warm[:], func=ACT.Exp)
+
+        warm_rows = consts.tile([P, SEQ], BF16)
+        nc.vector.memset(warm_rows[:], 0.0)
+
+        def keep_warm(passes):
+            warm_ps = psum_out.tile([P, SEQ], F32, name="out_ps")
+            for n in range(passes):
+                nc.tensor.matmul(out=warm_ps[:], lhsT=warm_rows[:, 0:P], rhs=warm_rows[:], start=True, stop=True)
+
+        keep_warm(WARM_PASSES)
 
         k_in, q_in, v_in = [], [], []
         for g in range(N_HEADS):
@@ -257,8 +269,12 @@ def tile_scaleddotproductattention_t_kernel(tc, query, key, value, attention_mas
                     write_mask_term(step + 1, j)
             if preparing and phase == 0:
                 transpose_rows("k", k_in[g], psum_words)
+                if g == 0:
+                    keep_warm(1)
             if preparing and phase == 2:
                 transpose_rows("q", q_in[g], psum_scores if g == 0 else psum_words)
+                if g == 0:
+                    keep_warm(1)
 
             if pair_ending_at(step - LAG_QUANTISE) is not None:
                 quantise_probs(pair_ending_at(step - LAG_QUANTISE))

@@ -189,9 +189,12 @@ def tile_scaleddotproductattention_t_kernel(tc, query, key, value, attention_mas
             nc.vector.reciprocal(out=inverse[:], in_=row_sum[i][:])
             inv_sum[i] = inverse
 
+        def on_vector(i):
+            return i % 2 == 0 or len(batches[batch_of[i]]) == 1
+
         def normalise(i):
             p_tile = work.tile([P, SEQ], BF16, name="probs")
-            if len(batches[batch_of[i]]) == 1:
+            if on_vector(i):
                 nc.vector.tensor_scalar(out=p_tile[:], in0=expo[i][:], scalar1=inv_sum[i][:], scalar2=None, op0=ALU.mult)
             else:
                 nc.gpsimd.tensor_scalar(
@@ -276,21 +279,23 @@ def tile_scaleddotproductattention_t_kernel(tc, query, key, value, attention_mas
                 if g == 0:
                     keep_warm(1)
 
+            vector_normalises = is_tile(step - LAG_NORMALISE) and on_vector(step - LAG_NORMALISE)
             if pair_ending_at(step - LAG_QUANTISE) is not None:
                 quantise_probs(pair_ending_at(step - LAG_QUANTISE))
+            if vector_normalises and is_tile(step - LAG_MAX):
+                row_max(step - LAG_MAX)
+            if is_tile(step - LAG_NORMALISE):
+                invert_sum(step - LAG_NORMALISE)
             if preparing and phase == 1:
                 regroup_value(g)
             if preparing and phase == 3:
                 quantise_value(g)
             if is_tile(step - LAG_NORMALISE):
-                invert_sum(step - LAG_NORMALISE)
-            if is_tile(step - LAG_MAX):
+                normalise(step - LAG_NORMALISE)
+            if not vector_normalises and is_tile(step - LAG_MAX):
                 row_max(step - LAG_MAX)
             if preparing and phase == 3:
                 copy_out_scaled_query(g)
-
-            if is_tile(step - LAG_NORMALISE):
-                normalise(step - LAG_NORMALISE)
 
             if is_tile(step - LAG_EXP):
                 exponentials(step - LAG_EXP)

@@ -190,7 +190,7 @@ def tile_scaleddotproductattention_t_kernel(tc, query, key, value, attention_mas
             inv_sum[i] = inverse
 
         def on_vector(i):
-            return i % 2 == 0 or len(batches[batch_of[i]]) == 1
+            return i % 2 == 0 or i >= N_TILES - 3
 
         def normalise(i):
             p_tile = work.tile([P, SEQ], BF16, name="probs")
@@ -282,6 +282,8 @@ def tile_scaleddotproductattention_t_kernel(tc, query, key, value, attention_mas
             vector_normalises = is_tile(step - LAG_NORMALISE) and on_vector(step - LAG_NORMALISE)
             if pair_ending_at(step - LAG_QUANTISE) is not None:
                 quantise_probs(pair_ending_at(step - LAG_QUANTISE))
+            if preparing and phase == 2:
+                quantise_value(g)
             if vector_normalises and is_tile(step - LAG_MAX):
                 row_max(step - LAG_MAX)
             if is_tile(step - LAG_NORMALISE):
@@ -289,13 +291,11 @@ def tile_scaleddotproductattention_t_kernel(tc, query, key, value, attention_mas
             if preparing and phase == 1:
                 regroup_value(g)
             if preparing and phase == 3:
-                quantise_value(g)
+                copy_out_scaled_query(g)
             if is_tile(step - LAG_NORMALISE):
                 normalise(step - LAG_NORMALISE)
             if not vector_normalises and is_tile(step - LAG_MAX):
                 row_max(step - LAG_MAX)
-            if preparing and phase == 3:
-                copy_out_scaled_query(g)
 
             if is_tile(step - LAG_EXP):
                 exponentials(step - LAG_EXP)

@@ -23,9 +23,10 @@ NEG_MIN = -3.4028234663852886e38
 
 FLOPS = 2 * (2 * N_HEADS * SEQ * SEQ * DIM)
 
-WARM_PASSES = 4
+WARM_PASSES = 5
 
 PREP_STEPS = 4
+LAG_VALUE = 8
 LAG_MAX = 1
 LAG_EXP = 2
 LAG_NORMALISE = 3
@@ -68,34 +69,37 @@ def tile_scaleddotproductattention_t_kernel(tc, query, key, value, attention_mas
         nc.vector.memset(warm[:], 0.0)
         nc.scalar.activation(out=warm[:], in_=warm[:], func=ACT.Exp)
 
-        warm_rows = consts.tile([P, SEQ], BF16)
+        warm_rows = consts.tile([P, P], F32)
         nc.vector.memset(warm_rows[:], 0.0)
 
         def keep_warm(passes):
-            warm_ps = psum_out.tile([P, SEQ], F32, name="out_ps")
+            warm_ps = psum_out.tile([P, P], F32, name="out_ps")
             for n in range(passes):
-                nc.tensor.matmul(out=warm_ps[:], lhsT=warm_rows[:, 0:P], rhs=warm_rows[:], start=True, stop=True)
+                nc.tensor.matmul(out=warm_ps[:], lhsT=warm_rows[:], rhs=warm_rows[:], start=True, stop=True)
 
         keep_warm(WARM_PASSES)
 
         k_in, q_in, v_in = [], [], []
         for g in range(N_HEADS):
             k_head = inputs.tile([P, PACK * DIM], BF16)
-            nc.sync.dma_start(out=k_head[:], in_=k_rows[g])
-            k_in.append(k_head)
             q_head = inputs.tile([P, PACK * DIM], BF16)
-            nc.sync.dma_start(out=q_head[:], in_=q_rows[g])
+            if g == 0:
+                nc.sync.dma_start(out=q_head[:, 0:DIM], in_=q_rows[g][:, 0:DIM])
+                nc.sync.dma_start(out=k_head[:], in_=k_rows[g])
+                nc.sync.dma_start(out=q_head[:, DIM:], in_=q_rows[g][:, DIM:])
+            else:
+                nc.sync.dma_start(out=k_head[:], in_=k_rows[g])
+                nc.sync.dma_start(out=q_head[:], in_=q_rows[g])
+            k_in.append(k_head)
             q_in.append(q_head)
             v_head = inputs.tile([P, PACK * DIM], BF16)
             nc.sync.dma_start(out=v_head[:], in_=v_rows[g])
             v_in.append(v_head)
 
         mask_term = consts.tile([P, BATCH * 2, 2], F32)
-        nc.vector.tensor_scalar(
+        nc.gpsimd.tensor_scalar(
             out=mask_term[:], in0=mask_in[:], scalar1=-NEG_MIN, scalar2=NEG_MIN, op0=ALU.mult, op1=ALU.add
         )
-        mask_termT = consts.tile([P, BATCH * 2, 2, P], F32)
-        nc.vector.tensor_copy(out=mask_termT[:], in_=mask_term[:].unsqueeze(3).to_broadcast([P, BATCH * 2, 2, P]))
 
         batches = [[i, i + 1] for i in range(0, N_TILES - 2, 2)] + [[N_TILES - 2], [N_TILES - 1]]
         batch_of = {}
@@ -107,9 +111,9 @@ def tile_scaleddotproductattention_t_kernel(tc, query, key, value, attention_mas
         z_ps, neg_max, expo, row_sum, inv_sum, probs, probsT_ps = {}, {}, {}, {}, {}, {}, {}
         p_grouped, p_codes, p_scales, out_ps = {}, {}, {}, {}
 
-        def transpose_rows(name, rows_in, pool):
+        def transpose_rows(name, rows_in):
             words = rows_in[:].bitcast(F32)
-            wordsT_ps = pool.tile([P, SEQ], F32, name="z_ps" if pool is psum_scores else "wordsT_ps")
+            wordsT_ps = psum_words.tile([P, SEQ], F32, name="wordsT_ps")
             for t in range(PACK):
                 cols = slice(t * P, (t + 1) * P)
                 nc.tensor.transpose(wordsT_ps[:, cols], words[:, cols], ident_f32[:])
@@ -154,7 +158,7 @@ def tile_scaleddotproductattention_t_kernel(tc, query, key, value, attention_mas
                 z_ps[i] = psum_scores.tile([P, SEQ], F32, name="z_ps")
             nc.tensor.matmul(
                 out=z_ps[i][:, j * P : (j + 1) * P],
-                lhsT=mask_termT[:, 2 * (i // (HEADS * Q_TILES)) + j % 2, j // 2, :],
+                lhsT=mask_term[:, 2 * (i // (HEADS * Q_TILES)) + j % 2, j // 2 : j // 2 + 1].to_broadcast([P, P]),
                 rhs=ident_f32[:],
                 is_transpose=True,
                 start=(j == 0),
@@ -255,9 +259,48 @@ def tile_scaleddotproductattention_t_kernel(tc, query, key, value, attention_mas
         def pair_ending_at(i):
             return batch_of[i] if is_tile(i) and batches[batch_of[i]][-1] == i else None
 
-        for step in range(-PREP_STEPS, N_TILES + LAG_STORE):
+        def prepare_first_head():
+            k_words = k_in[0][:].bitcast(F32)
+            q_words = q_in[0][:].bitcast(F32)
+            first_ps = psum_words.tile([P, SEQ], F32, name="wordsT_ps")
+            nc.tensor.transpose(first_ps[:, 0:P], q_words[:, 0:P], ident_f32[:])
+            halves = []
+            for u in range(2):
+                half = psum_probs.tile([P, 2, P], F32, name="probsT_ps")
+                for e in range(2):
+                    j = 2 * e + u
+                    nc.tensor.transpose(half[:, e, :], k_words[:, j * P : (j + 1) * P], ident_f32[:])
+                halves.append(half)
+            rest_ps = psum_scores.tile([P, SEQ], F32, name="z_ps")
+            for j in range(PACK):
+                write_mask_term(0, j)
+            for t in range(1, Q_TILES):
+                cols = slice(t * P, (t + 1) * P)
+                nc.tensor.transpose(rest_ps[:, cols], q_words[:, cols], ident_f32[:])
+
+            scaled = transposed.tile([P, 2 * SEQ], BF16, name="qT")
+            wordsT = transposed.tile([P, SEQ], F32, name="kT")
+            nc.vector.tensor_scalar(
+                out=scaled[:, 0:DIM], in0=first_ps[:, 0:P].bitcast(BF16), scalar1=SCALE, scalar2=None, op0=ALU.mult
+            )
+            nc.scalar.copy(
+                out=wordsT[:, 0:DIM].rearrange("w (p e) -> w p e", e=2), in_=halves[0][:].rearrange("w e p -> w p e")
+            )
+            nc.vector.tensor_copy(
+                out=wordsT[:, DIM:].rearrange("w (p e) -> w p e", e=2), in_=halves[1][:].rearrange("w e p -> w p e")
+            )
+            nc.vector.tensor_scalar(
+                out=scaled[:, DIM:], in0=rest_ps[:, P:].bitcast(BF16), scalar1=SCALE, scalar2=None, op0=ALU.mult
+            )
+            qT[0] = by_parity(scaled[:])
+            kT[0] = by_parity(wordsT[:].bitcast(BF16))
+
+        prepare_first_head()
+
+        for step in range(N_TILES + LAG_STORE):
             g, phase = divmod(step + PREP_STEPS, Q_TILES)
             preparing = g < N_HEADS
+            value_head = g - LAG_VALUE // Q_TILES
 
             if is_tile(step - LAG_TRANSPOSE):
                 transpose_probs(step - LAG_TRANSPOSE)
@@ -271,25 +314,21 @@ def tile_scaleddotproductattention_t_kernel(tc, query, key, value, attention_mas
                 for j in range(PACK):
                     write_mask_term(step + 1, j)
             if preparing and phase == 0:
-                transpose_rows("k", k_in[g], psum_words)
-                if g == 0:
-                    keep_warm(1)
+                transpose_rows("k", k_in[g])
             if preparing and phase == 2:
-                transpose_rows("q", q_in[g], psum_scores if g == 0 else psum_words)
-                if g == 0:
-                    keep_warm(1)
+                transpose_rows("q", q_in[g])
 
             vector_normalises = is_tile(step - LAG_NORMALISE) and on_vector(step - LAG_NORMALISE)
             if pair_ending_at(step - LAG_QUANTISE) is not None:
                 quantise_probs(pair_ending_at(step - LAG_QUANTISE))
-            if preparing and phase == 2:
-                quantise_value(g)
+            if phase == 2 and 0 <= value_head < N_HEADS:
+                quantise_value(value_head)
             if vector_normalises and is_tile(step - LAG_MAX):
                 row_max(step - LAG_MAX)
             if is_tile(step - LAG_NORMALISE):
                 invert_sum(step - LAG_NORMALISE)
-            if preparing and phase == 1:
-                regroup_value(g)
+            if phase == 1 and 0 <= value_head < N_HEADS:
+                regroup_value(value_head)
             if preparing and phase == 3:
                 copy_out_scaled_query(g)
             if is_tile(step - LAG_NORMALISE):

@@ -25,16 +25,20 @@ FLOPS = 2 * (2 * N_HEADS * SEQ * SEQ * DIM)
 
 WARM_PASSES = 5
 
-PREP_STEPS = 4
-LAG_VALUE = 8
 LAG_MAX = 1
-LAG_EXP = 2
+LAG_EXP = 1
 LAG_NORMALISE = 3
-LAG_TRANSPOSE = 5
-LAG_GROUP = 6
+LAG_TRANSPOSE = 4
 LAG_QUANTISE = 7
 LAG_ATTEND = 8
 LAG_STORE = 9
+LAG_KEY = -4
+LAG_QUERY = -2
+LAG_QUERY_COPY = -1
+LAG_VALUE = -2
+LAG_VALUE_CODES = 0
+FIRST_VALUE = 1
+SHARED_STORES = 6
 
 
 def tile_scaleddotproductattention_t_kernel(tc, query, key, value, attention_mask, out):
@@ -52,8 +56,9 @@ def tile_scaleddotproductattention_t_kernel(tc, query, key, value, attention_mas
         inputs = ctx.enter_context(tc.tile_pool(name="inputs", bufs=N_HEADS))
         transposed = ctx.enter_context(tc.tile_pool(name="transposed", bufs=2))
         work = ctx.enter_context(tc.tile_pool(name="work", bufs=4))
+        results = ctx.enter_context(tc.tile_pool(name="results", bufs=8))
         stats = ctx.enter_context(tc.tile_pool(name="stats", bufs=4))
-        packed = ctx.enter_context(tc.tile_pool(name="packed", bufs=2))
+        packed = ctx.enter_context(tc.tile_pool(name="packed", bufs=4))
         v_packed = ctx.enter_context(tc.tile_pool(name="v_packed", bufs=N_HEADS))
         psum_words = ctx.enter_context(tc.psum_pool(name="psum_words", bufs=1))
         psum_scores = ctx.enter_context(tc.psum_pool(name="psum_scores", bufs=4))
@@ -194,7 +199,7 @@ def tile_scaleddotproductattention_t_kernel(tc, query, key, value, attention_mas
             inv_sum[i] = inverse
 
         def on_vector(i):
-            return i % 2 == 0 or i >= N_TILES - 3
+            return i % 2 == 0 or i >= N_TILES - 2
 
         def normalise(i):
             p_tile = work.tile([P, SEQ], BF16, name="probs")
@@ -230,8 +235,8 @@ def tile_scaleddotproductattention_t_kernel(tc, query, key, value, attention_mas
 
         def attend(n):
             g = batches[n][0] // Q_TILES
-            if n == len(batches) - 1:
-                acc = psum_words.tile([P, len(batches[n]), DIM], F32, name="wordsT_ps")
+            if n >= len(batches) - 4:
+                acc = psum_scores.tile([P, len(batches[n]), DIM], F32, name="z_ps")
             else:
                 acc = psum_out.tile([P, len(batches[n]), DIM], F32, name="out_ps")
             for place in range(len(batches[n])):
@@ -249,15 +254,12 @@ def tile_scaleddotproductattention_t_kernel(tc, query, key, value, attention_mas
 
         def store(n):
             g, t = divmod(batches[n][0], Q_TILES)
-            result = work.tile([P, len(batches[n]), DIM], F32, name="out_sb")
-            nc.scalar.copy(out=result[:], in_=out_ps[n][:])
+            result = results.tile([P, len(batches[n]), DIM], F32, name="out_sb")
+            if n >= len(batches) - SHARED_STORES and n % 2 == 1:
+                nc.vector.tensor_copy(out=result[:], in_=out_ps[n][:])
+            else:
+                nc.scalar.copy(out=result[:], in_=out_ps[n][:])
             nc.sync.dma_start(out=out_rows[g][:, t : t + len(batches[n]), :], in_=result[:])
-
-        def is_tile(i):
-            return 0 <= i < N_TILES
-
-        def pair_ending_at(i):
-            return batch_of[i] if is_tile(i) and batches[batch_of[i]][-1] == i else None
 
         def prepare_first_head():
             k_words = k_in[0][:].bitcast(F32)
@@ -271,7 +273,7 @@ def tile_scaleddotproductattention_t_kernel(tc, query, key, value, attention_mas
                     j = 2 * e + u
                     nc.tensor.transpose(half[:, e, :], k_words[:, j * P : (j + 1) * P], ident_f32[:])
                 halves.append(half)
-            rest_ps = psum_scores.tile([P, SEQ], F32, name="z_ps")
+            rest_ps = psum_out.tile([P, SEQ], F32, name="out_ps")
             for j in range(PACK):
                 write_mask_term(0, j)
             for t in range(1, Q_TILES):
@@ -297,50 +299,58 @@ def tile_scaleddotproductattention_t_kernel(tc, query, key, value, attention_mas
 
         prepare_first_head()
 
+        def due(step, lag):
+            return [step - lag] if 0 <= step - lag < N_TILES else []
+
+        def batches_due(step, lag):
+            return [batch_of[i] for i in due(step, lag) if batches[batch_of[i]][-1] == i]
+
+        def heads_due(step, lag, first=1):
+            g, phase = divmod(step - lag, Q_TILES)
+            return [g] if phase == 0 and first <= g < N_HEADS else []
+
         for step in range(N_TILES + LAG_STORE):
-            g, phase = divmod(step + PREP_STEPS, Q_TILES)
-            preparing = g < N_HEADS
-            value_head = g - LAG_VALUE // Q_TILES
-
-            if is_tile(step - LAG_TRANSPOSE):
-                transpose_probs(step - LAG_TRANSPOSE)
-            if is_tile(step):
-                add_scores(step, 0)
-            if pair_ending_at(step - LAG_ATTEND) is not None:
-                attend(pair_ending_at(step - LAG_ATTEND))
-            if is_tile(step):
-                add_scores(step, 1)
-            if is_tile(step + 1):
-                for j in range(PACK):
-                    write_mask_term(step + 1, j)
-            if preparing and phase == 0:
-                transpose_rows("k", k_in[g])
-            if preparing and phase == 2:
+            for i in due(step, 0):
+                add_scores(i, 0)
+            for g in heads_due(step, LAG_QUERY):
                 transpose_rows("q", q_in[g])
+            for i in due(step, 0):
+                add_scores(i, 1)
+            for g in heads_due(step, LAG_KEY):
+                transpose_rows("k", k_in[g])
+            for n in batches_due(step, LAG_ATTEND):
+                attend(n)
+            for i in due(step, LAG_TRANSPOSE):
+                transpose_probs(i)
+            for i in due(step, -1):
+                if i > 0:
+                    for j in range(PACK):
+                        write_mask_term(i, j)
 
-            vector_normalises = is_tile(step - LAG_NORMALISE) and on_vector(step - LAG_NORMALISE)
-            if pair_ending_at(step - LAG_QUANTISE) is not None:
-                quantise_probs(pair_ending_at(step - LAG_QUANTISE))
-            if phase == 2 and 0 <= value_head < N_HEADS:
-                quantise_value(value_head)
-            if vector_normalises and is_tile(step - LAG_MAX):
-                row_max(step - LAG_MAX)
-            if is_tile(step - LAG_NORMALISE):
-                invert_sum(step - LAG_NORMALISE)
-            if phase == 1 and 0 <= value_head < N_HEADS:
-                regroup_value(value_head)
-            if preparing and phase == 3:
+            for g in heads_due(step, LAG_VALUE_CODES) if step > 0 else []:
+                quantise_value(g)
+            if step == FIRST_VALUE + 1:
+                quantise_value(0)
+            for n in batches_due(step, LAG_QUANTISE):
+                quantise_probs(n)
+            for i in due(step, LAG_NORMALISE):
+                invert_sum(i)
+            for g in heads_due(step, LAG_VALUE):
+                regroup_value(g)
+            if step == FIRST_VALUE:
+                regroup_value(0)
+            for g in heads_due(step, LAG_QUERY_COPY):
                 copy_out_scaled_query(g)
-            if is_tile(step - LAG_NORMALISE):
-                normalise(step - LAG_NORMALISE)
-            if not vector_normalises and is_tile(step - LAG_MAX):
-                row_max(step - LAG_MAX)
+            for i in due(step, LAG_MAX):
+                row_max(i)
+            for i in due(step, LAG_NORMALISE):
+                normalise(i)
 
-            if is_tile(step - LAG_EXP):
-                exponentials(step - LAG_EXP)
-            if is_tile(step - LAG_GROUP):
-                group_probs(step - LAG_GROUP)
-            if preparing and phase == 1:
+            for n in batches_due(step, LAG_STORE):
+                store(n)
+            for i in due(step, LAG_EXP):
+                exponentials(i)
+            for g in heads_due(step, LAG_KEY):
                 copy_out_key_words(g)
-            if pair_ending_at(step - LAG_STORE) is not None:
-                store(pair_ending_at(step - LAG_STORE))
+            for i in due(step, LAG_TRANSPOSE):
+                group_probs(i)

@@ -36,7 +36,7 @@ LAG_KEY = -4
 LAG_QUERY = -2
 LAG_QUERY_COPY = -1
 LAG_VALUE = -2
-LAG_VALUE_CODES = 0
+LAG_VALUE_CODES = 2
 FIRST_VALUE = 1
 SHARED_STORES = 6
 
@@ -89,8 +89,11 @@ def tile_scaleddotproductattention_t_kernel(tc, query, key, value, attention_mas
             k_head = inputs.tile([P, PACK * DIM], BF16)
             q_head = inputs.tile([P, PACK * DIM], BF16)
             if g == 0:
+                k_half_rows = k_rows[g].rearrange("p (e u d) -> p u e d", e=2, u=2)
+                k_halves = k_head[:].rearrange("p (u e d) -> p u e d", e=2, u=2)
+                nc.sync.dma_start(out=k_halves[:, 0], in_=k_half_rows[:, 0])
                 nc.sync.dma_start(out=q_head[:, 0:DIM], in_=q_rows[g][:, 0:DIM])
-                nc.sync.dma_start(out=k_head[:], in_=k_rows[g])
+                nc.sync.dma_start(out=k_halves[:, 1], in_=k_half_rows[:, 1])
                 nc.sync.dma_start(out=q_head[:, DIM:], in_=q_rows[g][:, DIM:])
             else:
                 nc.sync.dma_start(out=k_head[:], in_=k_rows[g])
@@ -170,14 +173,14 @@ def tile_scaleddotproductattention_t_kernel(tc, query, key, value, attention_mas
                 stop=False,
             )
 
-        def add_scores(i, parity):
+        def add_scores(i, parity, first=0, last=SEQ):
             g, t = divmod(i, Q_TILES)
             nc.tensor.matmul(
-                out=z_ps[i][:],
+                out=z_ps[i][:, first:last],
                 lhsT=qT[g][:, parity, t * P : (t + 1) * P],
-                rhs=kT[g][:, parity, :],
+                rhs=kT[g][:, parity, first:last],
                 start=False,
-                stop=(parity == 1),
+                stop=(parity == 1 and last == SEQ),
             )
 
         def row_max(i):
@@ -264,38 +267,40 @@ def tile_scaleddotproductattention_t_kernel(tc, query, key, value, attention_mas
         def prepare_first_head():
             k_words = k_in[0][:].bitcast(F32)
             q_words = q_in[0][:].bitcast(F32)
-            first_ps = psum_words.tile([P, SEQ], F32, name="wordsT_ps")
-            nc.tensor.transpose(first_ps[:, 0:P], q_words[:, 0:P], ident_f32[:])
-            halves = []
-            for u in range(2):
-                half = psum_probs.tile([P, 2, P], F32, name="probsT_ps")
-                for e in range(2):
-                    j = 2 * e + u
-                    nc.tensor.transpose(half[:, e, :], k_words[:, j * P : (j + 1) * P], ident_f32[:])
-                halves.append(half)
-            rest_ps = psum_out.tile([P, SEQ], F32, name="out_ps")
-            for j in range(PACK):
-                write_mask_term(0, j)
-            for t in range(1, Q_TILES):
-                cols = slice(t * P, (t + 1) * P)
-                nc.tensor.transpose(rest_ps[:, cols], q_words[:, cols], ident_f32[:])
-
             scaled = transposed.tile([P, 2 * SEQ], BF16, name="qT")
             wordsT = transposed.tile([P, SEQ], F32, name="kT")
+            qT[0] = by_parity(scaled[:])
+            kT[0] = by_parity(wordsT[:].bitcast(BF16))
+
+            def transpose_key_half(u):
+                half = psum_probs.tile([P, 2, P], F32, name="probsT_ps")
+                for e in range(2):
+                    j = 2 * u + e
+                    nc.tensor.transpose(half[:, e, :], k_words[:, j * P : (j + 1) * P], ident_f32[:])
+                return half[:].rearrange("w e p -> w p e"), wordsT[:, u * DIM : (u + 1) * DIM].rearrange("w (p e) -> w p e", e=2)
+
+            half_ps, half_out = transpose_key_half(0)
+            nc.scalar.copy(out=half_out, in_=half_ps)
+            first_ps = psum_words.tile([P, SEQ], F32, name="wordsT_ps")
+            nc.tensor.transpose(first_ps[:, 0:P], q_words[:, 0:P], ident_f32[:])
             nc.vector.tensor_scalar(
                 out=scaled[:, 0:DIM], in0=first_ps[:, 0:P].bitcast(BF16), scalar1=SCALE, scalar2=None, op0=ALU.mult
             )
-            nc.scalar.copy(
-                out=wordsT[:, 0:DIM].rearrange("w (p e) -> w p e", e=2), in_=halves[0][:].rearrange("w e p -> w p e")
-            )
-            nc.vector.tensor_copy(
-                out=wordsT[:, DIM:].rearrange("w (p e) -> w p e", e=2), in_=halves[1][:].rearrange("w e p -> w p e")
-            )
+            half_ps, half_out = transpose_key_half(1)
+            nc.vector.tensor_copy(out=half_out, in_=half_ps)
+            for j in range(PACK):
+                write_mask_term(0, j)
+            for parity in range(2):
+                add_scores(0, parity, 0, DIM)
+            rest_ps = psum_out.tile([P, SEQ], F32, name="out_ps")
+            for t in range(1, Q_TILES):
+                cols = slice(t * P, (t + 1) * P)
+                nc.tensor.transpose(rest_ps[:, cols], q_words[:, cols], ident_f32[:])
+            for parity in range(2):
+                add_scores(0, parity, DIM, SEQ)
             nc.vector.tensor_scalar(
                 out=scaled[:, DIM:], in0=rest_ps[:, P:].bitcast(BF16), scalar1=SCALE, scalar2=None, op0=ALU.mult
             )
-            qT[0] = by_parity(scaled[:])
-            kT[0] = by_parity(wordsT[:].bitcast(BF16))
 
         prepare_first_head()
 
@@ -311,11 +316,13 @@ def tile_scaleddotproductattention_t_kernel(tc, query, key, value, attention_mas
 
         for step in range(N_TILES + LAG_STORE):
             for i in due(step, 0):
-                add_scores(i, 0)
+                if i > 0:
+                    add_scores(i, 0)
             for g in heads_due(step, LAG_QUERY):
                 transpose_rows("q", q_in[g])
             for i in due(step, 0):
-                add_scores(i, 1)
+                if i > 0:
+                    add_scores(i, 1)
             for g in heads_due(step, LAG_KEY):
                 transpose_rows("k", k_in[g])
             for n in batches_due(step, LAG_ATTEND):
@@ -327,7 +334,7 @@ def tile_scaleddotproductattention_t_kernel(tc, query, key, value, attention_mas
                     for j in range(PACK):
                         write_mask_term(i, j)
 
-            for g in heads_due(step, LAG_VALUE_CODES) if step > 0 else []:
+            for g in heads_due(step, LAG_VALUE_CODES):
                 quantise_value(g)
             if step == FIRST_VALUE + 1:
                 quantise_value(0)

@@ -162,15 +162,15 @@ def tile_scaleddotproductattention_t_kernel(tc, query, key, value, attention_mas
             v_codes[g], v_scales[g] = codes, scales
 
         def write_mask_term(i, j):
-            if j == 0:
+            if j == 0 and i > 0:
                 z_ps[i] = psum_scores.tile([P, SEQ], F32, name="z_ps")
             nc.tensor.matmul(
                 out=z_ps[i][:, j * P : (j + 1) * P],
                 lhsT=mask_term[:, 2 * (i // (HEADS * Q_TILES)) + j % 2, j // 2 : j // 2 + 1].to_broadcast([P, P]),
                 rhs=ident_f32[:],
                 is_transpose=True,
-                start=(j == 0),
-                stop=False,
+                start=(j == 0 and i > 0),
+                stop=(j == PACK - 1 and i == 0),
             )
 
         def add_scores(i, parity, first=0, last=SEQ):
@@ -179,8 +179,8 @@ def tile_scaleddotproductattention_t_kernel(tc, query, key, value, attention_mas
                 out=z_ps[i][:, first:last],
                 lhsT=qT[g][:, parity, t * P : (t + 1) * P],
                 rhs=kT[g][:, parity, first:last],
-                start=False,
-                stop=(parity == 1 and last == SEQ),
+                start=(parity == 0 and first == 0 and i == 0),
+                stop=(parity == 1 and i > 0),
             )
 
         def row_max(i):
@@ -288,8 +288,7 @@ def tile_scaleddotproductattention_t_kernel(tc, query, key, value, attention_mas
             )
             half_ps, half_out = transpose_key_half(1)
             nc.vector.tensor_copy(out=half_out, in_=half_ps)
-            for j in range(PACK):
-                write_mask_term(0, j)
+            z_ps[0] = psum_scores.tile([P, SEQ], F32, name="z_ps")
             for parity in range(2):
                 add_scores(0, parity, 0, DIM)
             rest_ps = psum_out.tile([P, SEQ], F32, name="out_ps")
@@ -298,6 +297,8 @@ def tile_scaleddotproductattention_t_kernel(tc, query, key, value, attention_mas
                 nc.tensor.transpose(rest_ps[:, cols], q_words[:, cols], ident_f32[:])
             for parity in range(2):
                 add_scores(0, parity, DIM, SEQ)
+            for j in range(PACK):
+                write_mask_term(0, j)
             nc.vector.tensor_scalar(
                 out=scaled[:, DIM:], in0=rest_ps[:, P:].bitcast(BF16), scalar1=SCALE, scalar2=None, op0=ALU.mult
             )
@@ -318,15 +319,15 @@ def tile_scaleddotproductattention_t_kernel(tc, query, key, value, attention_mas
             for i in due(step, 0):
                 if i > 0:
                     add_scores(i, 0)
-            for g in heads_due(step, LAG_QUERY):
-                transpose_rows("q", q_in[g])
+            for n in batches_due(step, LAG_ATTEND):
+                attend(n)
             for i in due(step, 0):
                 if i > 0:
                     add_scores(i, 1)
+            for g in heads_due(step, LAG_QUERY):
+                transpose_rows("q", q_in[g])
             for g in heads_due(step, LAG_KEY):
                 transpose_rows("k", k_in[g])
-            for n in batches_due(step, LAG_ATTEND):
-                attend(n)
             for i in due(step, LAG_TRANSPOSE):
                 transpose_probs(i)
             for i in due(step, -1):

@@ -38,7 +38,7 @@ LAG_QUERY_COPY = -1
 LAG_VALUE = -2
 LAG_VALUE_CODES = 2
 FIRST_VALUE = 1
-SHARED_STORES = 6
+VS = (22, 26, 30)
 
 
 def tile_scaleddotproductattention_t_kernel(tc, query, key, value, attention_mask, out):
@@ -258,7 +258,7 @@ def tile_scaleddotproductattention_t_kernel(tc, query, key, value, attention_mas
         def store(n):
             g, t = divmod(batches[n][0], Q_TILES)
             result = results.tile([P, len(batches[n]), DIM], F32, name="out_sb")
-            if n >= len(batches) - SHARED_STORES and n % 2 == 1:
+            if batches[n][0] in VS:
                 nc.vector.tensor_copy(out=result[:], in_=out_ps[n][:])
             else:
                 nc.scalar.copy(out=result[:], in_=out_ps[n][:])
@@ -319,8 +319,12 @@ def tile_scaleddotproductattention_t_kernel(tc, query, key, value, attention_mas
             for i in due(step, 0):
                 if i > 0:
                     add_scores(i, 0)
-            for n in batches_due(step, LAG_ATTEND):
+            attending = batches_due(step, LAG_ATTEND)
+            for n in attending:
                 attend(n)
+            for i in due(step, -1):
+                if i > 0 and not attending:
+                    write_mask_term(i, 0)
             for i in due(step, 0):
                 if i > 0:
                     add_scores(i, 1)
@@ -332,7 +336,7 @@ def tile_scaleddotproductattention_t_kernel(tc, query, key, value, attention_mas
                 transpose_probs(i)
             for i in due(step, -1):
                 if i > 0:
-                    for j in range(PACK):
+                    for j in range(0 if attending else 1, PACK):
                         write_mask_term(i, j)
 
             for g in heads_due(step, LAG_VALUE_CODES):
@@ -342,7 +346,8 @@ def tile_scaleddotproductattention_t_kernel(tc, query, key, value, attention_mas
             for n in batches_due(step, LAG_QUANTISE):
                 quantise_probs(n)
             for i in due(step, LAG_NORMALISE):
-                invert_sum(i)
+                if i < N_TILES - 2:
+                    invert_sum(i)
             for g in heads_due(step, LAG_VALUE):
                 regroup_value(g)
             if step == FIRST_VALUE:
@@ -353,6 +358,9 @@ def tile_scaleddotproductattention_t_kernel(tc, query, key, value, attention_mas
                 row_max(i)
             for i in due(step, LAG_NORMALISE):
                 normalise(i)
+            for i in due(step, LAG_NORMALISE - 1):
+                if i >= N_TILES - 2:
+                    invert_sum(i)
 
             for n in batches_due(step, LAG_STORE):
                 store(n)

from contextlib import ExitStack

import concourse.mybir as mybir
from concourse.masks import make_identity

F32 = mybir.dt.float32
BF16 = mybir.dt.bfloat16
U32 = mybir.dt.uint32
U8 = mybir.dt.uint8
FP8X4 = mybir.dt.float8_e4m3fn_x4
ALU = mybir.AluOpType
ACT = mybir.ActivationFunctionType
AXIS = mybir.AxisListType

P = 128
PACK = 4
BATCH, HEADS, SEQ, DIM = 2, 4, 512, 256
N_HEADS = BATCH * HEADS
Q_TILES = SEQ // P
N_TILES = N_HEADS * Q_TILES
SCALE = 1.0 / 16.0
NEG_MIN = -3.4028234663852886e38

FLOPS = 2 * (2 * N_HEADS * SEQ * SEQ * DIM)

WARM_PASSES = 5

LAG_MAX = 1
LAG_EXP = 1
LAG_NORMALISE = 3
LAG_TRANSPOSE = 4
LAG_QUANTISE = 7
LAG_ATTEND = 8
LAG_STORE = 9
LAG_KEY = -4
LAG_QUERY = -2
LAG_QUERY_COPY = -1
LAG_VALUE = -2
LAG_VALUE_CODES = 2
FIRST_VALUE = 1
VS = (22, 26, 30)


def tile_scaleddotproductattention_t_kernel(tc, query, key, value, attention_mask, out):
    nc = tc.nc

    q_rows = query.rearrange("b h (p t) d -> (b h) p (t d)", t=PACK)
    k_rows = key.rearrange("b h (p j) d -> (b h) p (j d)", j=PACK)
    v_rows = value.rearrange("b h (p j) d -> (b h) p (j d)", j=PACK)
    out_rows = out.rearrange("b h (p t) d -> (b h) p t d", t=PACK)
    mask_cols = attention_mask.rearrange("b x y (h c u) -> c (b x y h) u", h=2, u=2)

    with ExitStack() as ctx:
        ctx.enter_context(tc.manual_schedule())
        consts = ctx.enter_context(tc.tile_pool(name="consts", bufs=1))
        inputs = ctx.enter_context(tc.tile_pool(name="inputs", bufs=N_HEADS))
        transposed = ctx.enter_context(tc.tile_pool(name="transposed", bufs=2))
        work = ctx.enter_context(tc.tile_pool(name="work", bufs=4))
        results = ctx.enter_context(tc.tile_pool(name="results", bufs=8))
        stats = ctx.enter_context(tc.tile_pool(name="stats", bufs=4))
        packed = ctx.enter_context(tc.tile_pool(name="packed", bufs=4))
        v_packed = ctx.enter_context(tc.tile_pool(name="v_packed", bufs=N_HEADS))
        psum_words = ctx.enter_context(tc.psum_pool(name="psum_words", bufs=1))
        psum_scores = ctx.enter_context(tc.psum_pool(name="psum_scores", bufs=4))
        psum_probs = ctx.enter_context(tc.psum_pool(name="psum_probs", bufs=2))
        psum_out = ctx.enter_context(tc.psum_pool(name="psum_out", bufs=1))

        ident_f32 = consts.tile([P, P], F32)
        make_identity(nc, ident_f32[:])
        mask_in = consts.tile([P, BATCH * 2, 2], BF16)
        with nc.allow_non_contiguous_dma(reason="2 KiB of mask, 4 bytes at a time"):
            nc.scalar.dma_start(out=mask_in[:], in_=mask_cols)
        warm = consts.tile([P, 1], F32)
        nc.vector.memset(warm[:], 0.0)
        nc.scalar.activation(out=warm[:], in_=warm[:], func=ACT.Exp)

        warm_rows = consts.tile([P, P], F32)
        nc.vector.memset(warm_rows[:], 0.0)

        def keep_warm(passes):
            warm_ps = psum_out.tile([P, P], F32, name="out_ps")
            for n in range(passes):
                nc.tensor.matmul(out=warm_ps[:], lhsT=warm_rows[:], rhs=warm_rows[:], start=True, stop=True)

        keep_warm(WARM_PASSES)

        k_in, q_in, v_in = [], [], []
        for g in range(N_HEADS):
            k_head = inputs.tile([P, PACK * DIM], BF16)
            q_head = inputs.tile([P, PACK * DIM], BF16)
            if g == 0:
                k_half_rows = k_rows[g].rearrange("p (e u d) -> p u e d", e=2, u=2)
                k_halves = k_head[:].rearrange("p (u e d) -> p u e d", e=2, u=2)
                nc.sync.dma_start(out=k_halves[:, 0], in_=k_half_rows[:, 0])
                nc.sync.dma_start(out=q_head[:, 0:DIM], in_=q_rows[g][:, 0:DIM])
                nc.sync.dma_start(out=k_halves[:, 1], in_=k_half_rows[:, 1])
                nc.sync.dma_start(out=q_head[:, DIM:], in_=q_rows[g][:, DIM:])
            else:
                nc.sync.dma_start(out=k_head[:], in_=k_rows[g])
                nc.sync.dma_start(out=q_head[:], in_=q_rows[g])
            k_in.append(k_head)
            q_in.append(q_head)
            v_head = inputs.tile([P, PACK * DIM], BF16)
            nc.sync.dma_start(out=v_head[:], in_=v_rows[g])
            v_in.append(v_head)

        mask_term = consts.tile([P, BATCH * 2, 2], F32)
        nc.gpsimd.tensor_scalar(
            out=mask_term[:], in0=mask_in[:], scalar1=-NEG_MIN, scalar2=NEG_MIN, op0=ALU.mult, op1=ALU.add
        )

        batches = [[i, i + 1] for i in range(0, N_TILES - 2, 2)] + [[N_TILES - 2], [N_TILES - 1]]
        batch_of = {}
        for n, tiles in enumerate(batches):
            for i in tiles:
                batch_of[i] = n

        words_ps, kT, qT, v_grouped, v_codes, v_scales = {}, {}, {}, {}, {}, {}
        z_ps, neg_max, expo, row_sum, inv_sum, probs, probsT_ps = {}, {}, {}, {}, {}, {}, {}
        p_grouped, p_codes, p_scales, out_ps = {}, {}, {}, {}

        def transpose_rows(name, rows_in):
            words = rows_in[:].bitcast(F32)
            wordsT_ps = psum_words.tile([P, SEQ], F32, name="wordsT_ps")
            for t in range(PACK):
                cols = slice(t * P, (t + 1) * P)
                nc.tensor.transpose(wordsT_ps[:, cols], words[:, cols], ident_f32[:])
            words_ps[name] = wordsT_ps

        def by_parity(pairs):
            return pairs.rearrange("w (c e) -> w e c", e=2)

        def copy_out_key_words(g):
            wordsT = transposed.tile([P, SEQ], F32, name="kT")
            nc.scalar.copy(
                out=wordsT[:].rearrange("w (u p e) -> w u p e", u=2, e=2),
                in_=words_ps["k"][:].rearrange("w (e u p) -> w u p e", u=2, e=2),
            )
            kT[g] = by_parity(wordsT[:].bitcast(BF16))

        def copy_out_scaled_query(g):
            scaled = transposed.tile([P, 2 * SEQ], BF16, name="qT")
            nc.vector.tensor_scalar(
                out=scaled[:], in0=words_ps["q"][:].bitcast(BF16), scalar1=SCALE, scalar2=None, op0=ALU.mult
            )
            qT[g] = by_parity(scaled[:])

        def regroup_value(g):
            grouped = packed.tile([P, DIM, PACK], BF16, name="v_grouped", align_bytes=64)
            nc.vector.tensor_copy(
                out=grouped[:].rearrange("p d (u e) -> p d u e", u=2),
                in_=v_in[g][:].rearrange("p (e u d) -> p d u e", e=2, u=2),
            )
            v_grouped[g] = grouped

        def quantise_value(g):
            codes = v_packed.tile([P, DIM], U32, name="v_codes", align_bytes=64)
            scales = v_packed.tile([P, DIM], U8, name="v_scales", align_bytes=64)
            nc.vector.quantize_mx(
                out=codes[:].bitcast(FP8X4), scales=scales[:], in_=v_grouped[g][:].rearrange("p d j -> p (d j)")
            )
            v_codes[g], v_scales[g] = codes, scales

        def write_mask_term(i, j):
            if j == 0 and i > 0:
                z_ps[i] = psum_scores.tile([P, SEQ], F32, name="z_ps")
            nc.tensor.matmul(
                out=z_ps[i][:, j * P : (j + 1) * P],
                lhsT=mask_term[:, 2 * (i // (HEADS * Q_TILES)) + j % 2, j // 2 : j // 2 + 1].to_broadcast([P, P]),
                rhs=ident_f32[:],
                is_transpose=True,
                start=(j == 0 and i > 0),
                stop=(j == PACK - 1 and i == 0),
            )

        def add_scores(i, parity, first=0, last=SEQ):
            g, t = divmod(i, Q_TILES)
            nc.tensor.matmul(
                out=z_ps[i][:, first:last],
                lhsT=qT[g][:, parity, t * P : (t + 1) * P],
                rhs=kT[g][:, parity, first:last],
                start=(parity == 0 and first == 0 and i == 0),
                stop=(parity == 1 and i > 0),
            )

        def row_max(i):
            negated = stats.tile([P, 1], F32, name="neg_max")
            nc.vector.tensor_reduce(out=negated[:], in_=z_ps[i][:], axis=AXIS.X, op=ALU.max, negate=True)
            neg_max[i] = negated

        def exponentials(i):
            e_tile = work.tile([P, SEQ], F32, name="expo")
            total = stats.tile([P, 1], F32, name="row_sum")
            nc.scalar.activation(
                out=e_tile[:], in_=z_ps[i][:], func=ACT.Exp, bias=neg_max[i][:], scale=1.0, accum_out=total[:]
            )
            expo[i], row_sum[i] = e_tile, total

        def invert_sum(i):
            inverse = stats.tile([P, 1], F32, name="inv_sum")
            nc.vector.reciprocal(out=inverse[:], in_=row_sum[i][:])
            inv_sum[i] = inverse

        def on_vector(i):
            return i % 2 == 0 or i >= N_TILES - 2

        def normalise(i):
            p_tile = work.tile([P, SEQ], BF16, name="probs")
            if on_vector(i):
                nc.vector.tensor_scalar(out=p_tile[:], in0=expo[i][:], scalar1=inv_sum[i][:], scalar2=None, op0=ALU.mult)
            else:
                nc.gpsimd.tensor_scalar(
                    out=p_tile[:], in0=expo[i][:], scalar1=inv_sum[i][:], scalar2=0.0, op0=ALU.mult, op1=ALU.add
                )
            probs[i] = p_tile

        def transpose_probs(i):
            words = probs[i][:].bitcast(F32)
            pT = psum_probs.tile([P, 2, P], F32, name="probsT_ps")
            for u in range(2):
                nc.tensor.transpose(pT[:, u, :], words[:, u * P : (u + 1) * P], ident_f32[:])
            probsT_ps[i] = pT

        def group_probs(i):
            n = batch_of[i]
            place = batches[n].index(i)
            if place == 0:
                p_grouped[n] = packed.tile([P, len(batches[n]), P, 2], F32, name="p_grouped", align_bytes=64)
            nc.scalar.copy(out=p_grouped[n][:, place], in_=probsT_ps[i][:].rearrange("p u q -> p q u"))

        def quantise_probs(n):
            codes = packed.tile([P, len(batches[n]) * P], U32, name="p_codes", align_bytes=64)
            scales = packed.tile([P, len(batches[n]) * P], U8, name="p_scales", align_bytes=64)
            nc.vector.quantize_mx(
                out=codes[:].bitcast(FP8X4), scales=scales[:], in_=p_grouped[n][:].rearrange("p a q u -> p (a q u)").bitcast(BF16)
            )
            p_codes[n], p_scales[n] = codes, scales

        def attend(n):
            g = batches[n][0] // Q_TILES
            if n >= len(batches) - 4:
                acc = psum_scores.tile([P, len(batches[n]), DIM], F32, name="z_ps")
            else:
                acc = psum_out.tile([P, len(batches[n]), DIM], F32, name="out_ps")
            for place in range(len(batches[n])):
                cols = slice(place * P, (place + 1) * P)
                nc.tensor.matmul_mx(
                    out=acc[:, place, :],
                    lhsT=p_codes[n][:, cols].bitcast(FP8X4),
                    lhsT_scale=p_scales[n][:, cols],
                    rhs=v_codes[g][:].bitcast(FP8X4),
                    rhs_scale=v_scales[g][:],
                    start=True,
                    stop=True,
                )
            out_ps[n] = acc

        def store(n):
            g, t = divmod(batches[n][0], Q_TILES)
            result = results.tile([P, len(batches[n]), DIM], F32, name="out_sb")
            if batches[n][0] in VS:
                nc.vector.tensor_copy(out=result[:], in_=out_ps[n][:])
            else:
                nc.scalar.copy(out=result[:], in_=out_ps[n][:])
            nc.sync.dma_start(out=out_rows[g][:, t : t + len(batches[n]), :], in_=result[:])

        def prepare_first_head():
            k_words = k_in[0][:].bitcast(F32)
            q_words = q_in[0][:].bitcast(F32)
            scaled = transposed.tile([P, 2 * SEQ], BF16, name="qT")
            wordsT = transposed.tile([P, SEQ], F32, name="kT")
            qT[0] = by_parity(scaled[:])
            kT[0] = by_parity(wordsT[:].bitcast(BF16))

            def transpose_key_half(u):
                half = psum_probs.tile([P, 2, P], F32, name="probsT_ps")
                for e in range(2):
                    j = 2 * u + e
                    nc.tensor.transpose(half[:, e, :], k_words[:, j * P : (j + 1) * P], ident_f32[:])
                return half[:].rearrange("w e p -> w p e"), wordsT[:, u * DIM : (u + 1) * DIM].rearrange("w (p e) -> w p e", e=2)

            half_ps, half_out = transpose_key_half(0)
            nc.scalar.copy(out=half_out, in_=half_ps)
            first_ps = psum_words.tile([P, SEQ], F32, name="wordsT_ps")
            nc.tensor.transpose(first_ps[:, 0:P], q_words[:, 0:P], ident_f32[:])
            nc.vector.tensor_scalar(
                out=scaled[:, 0:DIM], in0=first_ps[:, 0:P].bitcast(BF16), scalar1=SCALE, scalar2=None, op0=ALU.mult
            )
            half_ps, half_out = transpose_key_half(1)
            nc.vector.tensor_copy(out=half_out, in_=half_ps)
            z_ps[0] = psum_scores.tile([P, SEQ], F32, name="z_ps")
            for parity in range(2):
                add_scores(0, parity, 0, DIM)
            rest_ps = psum_out.tile([P, SEQ], F32, name="out_ps")
            for t in range(1, Q_TILES):
                cols = slice(t * P, (t + 1) * P)
                nc.tensor.transpose(rest_ps[:, cols], q_words[:, cols], ident_f32[:])
            for parity in range(2):
                add_scores(0, parity, DIM, SEQ)
            for j in range(PACK):
                write_mask_term(0, j)
            nc.vector.tensor_scalar(
                out=scaled[:, DIM:], in0=rest_ps[:, P:].bitcast(BF16), scalar1=SCALE, scalar2=None, op0=ALU.mult
            )

        prepare_first_head()

        def due(step, lag):
            return [step - lag] if 0 <= step - lag < N_TILES else []

        def batches_due(step, lag):
            return [batch_of[i] for i in due(step, lag) if batches[batch_of[i]][-1] == i]

        def heads_due(step, lag, first=1):
            g, phase = divmod(step - lag, Q_TILES)
            return [g] if phase == 0 and first <= g < N_HEADS else []

        for step in range(N_TILES + LAG_STORE):
            for i in due(step, 0):
                if i > 0:
                    add_scores(i, 0)
            attending = batches_due(step, LAG_ATTEND)
            for n in attending:
                attend(n)
            for i in due(step, -1):
                if i > 0 and not attending:
                    write_mask_term(i, 0)
            for i in due(step, 0):
                if i > 0:
                    add_scores(i, 1)
            for g in heads_due(step, LAG_QUERY):
                transpose_rows("q", q_in[g])
            for g in heads_due(step, LAG_KEY):
                transpose_rows("k", k_in[g])
            for i in due(step, LAG_TRANSPOSE):
                transpose_probs(i)
            for i in due(step, -1):
                if i > 0:
                    for j in range(0 if attending else 1, PACK):
                        write_mask_term(i, j)

            for g in heads_due(step, LAG_VALUE_CODES):
                quantise_value(g)
            if step == FIRST_VALUE + 1:
                quantise_value(0)
            for n in batches_due(step, LAG_QUANTISE):
                quantise_probs(n)
            for i in due(step, LAG_NORMALISE):
                if i < N_TILES - 2:
                    invert_sum(i)
            for g in heads_due(step, LAG_VALUE):
                regroup_value(g)
            if step == FIRST_VALUE:
                regroup_value(0)
            for g in heads_due(step, LAG_QUERY_COPY):
                copy_out_scaled_query(g)
            for i in due(step, LAG_MAX):
                row_max(i)
            for i in due(step, LAG_NORMALISE):
                normalise(i)
            for i in due(step, LAG_NORMALISE - 1):
                if i >= N_TILES - 2:
                    invert_sum(i)

            for n in batches_due(step, LAG_STORE):
                store(n)
            for i in due(step, LAG_EXP):
                exponentials(i)
            for g in heads_due(step, LAG_KEY):
                copy_out_key_words(g)
            for i in due(step, LAG_TRANSPOSE):
                group_probs(i)
